import numpy as np
import ml_dtypes


def mxq(x, axis, fmt="e4m3"):
    dtype, down = {"e4m3": (ml_dtypes.float8_e4m3fn, 7), "e5m2": (ml_dtypes.float8_e5m2, 14)}[fmt]
    v = np.moveaxis(np.asarray(x, np.float32).astype(ml_dtypes.bfloat16).astype(np.float64), axis, -1)
    blocks = v.reshape(v.shape[:-1] + (-1, 32))
    amax = np.abs(blocks).max(-1, keepdims=True)
    byte = np.maximum(np.where(amax > 0, np.frexp(amax)[1] - 1 + 127, 0) - down, 1)
    scale = np.exp2(byte - 127.0)
    codes = (blocks / scale).astype(np.float32).astype(dtype).astype(np.float64)
    return np.moveaxis((codes * scale).reshape(v.shape), -1, axis)


WIDE = False


def mx_kscale(k):
    if not WIDE:
        return np.ones(k)
    levels = np.array([10, -10, 5, -5, 0])
    a = np.random.permutation(np.resize(levels, k // 512 * 4)).reshape(k // 512, 4)
    idx = np.arange(k)
    return np.exp2(a[idx // 512, idx % 128 // 32])


BF16 = ml_dtypes.bfloat16


def bf(x):
    return np.asarray(x, np.float32).astype(BF16)


def f64(x):
    return np.asarray(x).astype(np.float64)


N, M, C, IMG = 1024, 2048, 1024, 256
NEG = -1e9
MAX_DISP = 192.0
V_TOL = 3.0


def draw_kpts(n):
    return bf(np.stack([np.random.randint(0, IMG, n), np.random.randint(0, IMG, n)], axis=1))


def setup_inputs():
    t = mx_kscale(C)
    return {"Q": bf(np.random.standard_normal((N, C))),
            "K": bf(np.random.standard_normal((M, C))),
            "V": bf(np.random.standard_normal((M, C)) * t[None, :]),
            "kpts_L": draw_kpts(N),
            "kpts_R": draw_kpts(M),
            "Wm": bf(np.random.standard_normal((C, C)) / np.sqrt(C) / t[None, :]),
            "bm": bf(np.random.standard_normal(C) * 0.1)}


def reference(Q, K, V, kpts_L, kpts_R, Wm, bm):
    pl, pr = f64(kpts_L), f64(kpts_R)
    dist_v = np.abs(pl[:, 1:2] - pr[:, 1][None, :])
    dist_u = pl[:, 0:1] - pr[:, 0][None, :]
    mask = (dist_v < V_TOL) & (dist_u > 0) & (dist_u < MAX_DISP)
    attn = f64(Q) @ f64(K).T * (1.0 / np.sqrt(C))
    attn = np.where(mask, attn, NEG)
    e = np.exp(attn - attn.max(-1, keepdims=True))
    esum = e.sum(-1, keepdims=True)
    matched = (mxq(e, 1, "e4m3") @ mxq(f64(V), 0, "e4m3")) / esum
    return (mxq(matched, 1, "e4m3") @ mxq(f64(Wm), 1, "e4m3").T) + f64(bm)

@@ -1,0 +1,430 @@
+from contextlib import ExitStack
+
+import concourse.mybir as mybir
+from concourse.masks import make_identity
+
+BF16 = mybir.dt.bfloat16
+F32 = mybir.dt.float32
+U32 = mybir.dt.uint32
+U8 = mybir.dt.uint8
+FP8X4 = mybir.dt.float8_e4m3fn_x4
+ALU = mybir.AluOpType
+ACT = mybir.ActivationFunctionType
+AXIS = mybir.AxisListType
+
+P = 128
+N_Q = 1024
+N_K = 2048
+C = 1024
+NT = N_Q // P
+CB = C // P
+BANK = 512
+NJ = N_K // BANK
+K_PASS = 512
+NG = N_K // K_PASS
+NF = C // K_PASS
+HALF = N_K // 2
+LAG = 3
+
+FLOPS = 2 * N_Q * N_K * C + 2 * N_Q * N_K * C + 2 * N_Q * C * C
+
+V_TOL = 3.0
+MAX_DISP = 192.0
+REACH = MAX_DISP / 2.0
+V_STRETCH = REACH / V_TOL
+SHRINK = 2.0 ** -40
+GROW = 2.0 ** 35
+
+
+def tile_epipolarcrossattention_pa_kernel(tc, Q, K, V, kpts_L, kpts_R, Wm, bm, out):
+    nc = tc.nc
+    with ExitStack() as ctx:
+        keep = ctx.enter_context(tc.tile_pool(name="keep", bufs=1))
+        raw = ctx.enter_context(tc.tile_pool(name="raw", bufs=5))
+        q_in = ctx.enter_context(tc.tile_pool(name="q_in", bufs=3))
+        two = ctx.enter_context(tc.tile_pool(name="two", bufs=2))
+        three = ctx.enter_context(tc.tile_pool(name="three", bufs=3))
+        ps_score = ctx.enter_context(tc.psum_pool(name="ps_score", bufs=2))
+        ps_turn = ctx.enter_context(tc.psum_pool(name="ps_turn", bufs=3))
+        ps_mx = ctx.enter_context(tc.psum_pool(name="ps_mx", bufs=3))
+        ctx.enter_context(tc.manual_schedule())
+
+        q_rows = Q.rearrange("(p i) c -> i p c", i=NT)
+        out_rows = out.rearrange("(p i) o -> i p o", i=NT)
+        k_rows = K.rearrange("(j b p) c -> j p b c", b=4, p=P)
+        w_rows = Wm.rearrange("(h b p) c -> h p b c", b=4, p=P)
+        v_rows = V.rearrange("(g u q e) c -> g q u e c", u=2, q=P, e=2)
+
+        q_raw = {}
+        k_raw = {}
+        w_raw = {}
+        v_raw = {}
+
+        def load_queries(i):
+            q_raw[i] = q_in.tile([P, C], BF16, name="q_raw")
+            nc.sync.dma_start(out=q_raw[i][:], in_=q_rows[i])
+
+        left = keep.tile([P, NT, 2], BF16)
+        nc.sync.dma_start(out=left[:], in_=kpts_L.rearrange("(p i) c -> p i c", i=NT))
+        load_queries(0)
+        right = keep.tile([P, N_K, 2], BF16)
+        for j in range(NJ):
+            k_raw[j] = raw.tile([P, 4, C], BF16, name="k_raw", tag="raw")
+            for b in range(4):
+                nc.sync.dma_start(out=k_raw[j][:, b, :], in_=k_rows[j][:, b, :])
+            if j == 0:
+                nc.sync.dma_start(
+                    out=right[:].rearrange("p m c -> p (m c)"),
+                    in_=kpts_R.rearrange("m c -> (m c)").partition_broadcast(P),
+                )
+        load_queries(1)
+        for g in range(NG):
+            v_raw[g] = raw.tile([P, 4, C], BF16, name="v_raw", tag="raw")
+            nc.sync.dma_start(
+                out=v_raw[g][:].rearrange("p (u e) c -> p u e c", u=2), in_=v_rows[g]
+            )
+        load_queries(2)
+        for h in range(2):
+            w_raw[h] = raw.tile([P, 4, C], BF16, name="w_raw", tag="raw")
+            nc.sync.dma_start(out=w_raw[h][:], in_=w_rows[h])
+        bias = keep.tile([P, C], BF16)
+        nc.sync.dma_start(out=bias[:], in_=bm.partition_broadcast(P))
+        for i in range(3, NT):
+            load_queries(i)
+
+        ident_bf = keep.tile([P, P], BF16)
+        make_identity(nc, ident_bf[:])
+        ident_f32 = keep.tile([P, P], F32)
+        make_identity(nc, ident_f32[:])
+        ones = keep.tile([P, P], F32)
+        nc.vector.memset(ones[:], 1.0)
+        shift_v = keep.tile([P, NT], F32)
+        nc.vector.tensor_scalar(
+            out=shift_v[:], in0=left[:, :, 1], scalar1=-V_STRETCH, scalar2=None, op0=ALU.mult
+        )
+        shift_u = keep.tile([P, NT], F32)
+        nc.vector.tensor_scalar(
+            out=shift_u[:], in0=left[:, :, 0], scalar1=-1.0, scalar2=REACH,
+            op0=ALU.mult, op1=ALU.add,
+        )
+
+        kT = keep.tile([P, CB, N_K], BF16)
+        v_codes = keep.tile([P, NG, C], U32, align_bytes=64)
+        v_scales = keep.tile([P, NG, C], U8, align_bytes=64)
+        w_codes = keep.tile([P, NF, C], U32, align_bytes=64)
+        w_scales = keep.tile([P, NF, C], U8, align_bytes=64)
+
+        qT = {}
+        far_v = {}
+        far_u = {}
+        cap = {}
+        y = {}
+        chunk_max = {}
+        exp_bias = {}
+        e = {}
+        half_sum = {}
+        spread = {}
+        e_grouped = {}
+        e_codes = {}
+        e_scales = {}
+        inv_sum = {}
+        m_grouped = {}
+        m_codes = {}
+        m_scales = {}
+        w_grouped = {}
+        v_grouped = {}
+        score_bank = {}
+
+        def turn_keys(j, piece):
+            b, half = piece // 2, piece % 2
+            bank = ps_turn.tile([P, 4, P], BF16, tag="turn")
+            for t in range(4):
+                cb = 4 * half + t
+                nc.tensor.transpose(bank[:, t, :], k_raw[j][:, b, cb * P:(cb + 1) * P], ident_bf[:])
+            dst = kT[:, 4 * half:4 * half + 4, j * BANK + b * P:j * BANK + (b + 1) * P]
+            nc.vector.tensor_copy(out=dst, in_=bank[:])
+
+        def turn_queries(i, half):
+            if half == 0:
+                qT[i] = two.tile([P, CB, P], BF16, name="qT")
+            bank = ps_turn.tile([P, 4, P], BF16, tag="turn")
+            for t in range(4):
+                cb = 4 * half + t
+                nc.tensor.transpose(bank[:, t, :], q_raw[i][:, cb * P:(cb + 1) * P], ident_bf[:])
+            nc.scalar.copy(out=qT[i][:, 4 * half:4 * half + 4, :], in_=bank[:])
+
+        def turn_weights(b):
+            words = w_raw[b // 4][:, b % 4, :].bitcast(F32)
+            bank = ps_turn.tile([P, 4, P], F32, tag="turn")
+            for t in range(4):
+                nc.tensor.transpose(bank[:, t, :], words[:, t * P:(t + 1) * P], ident_f32[:])
+            for f in range(NF):
+                nc.scalar.copy(
+                    out=w_grouped[f][:].bitcast(F32).rearrange("p (o u) -> p o u", u=2)[
+                        :, b * P:(b + 1) * P, :
+                    ],
+                    in_=bank[:, 2 * f:2 * f + 2, :].rearrange("p u o -> p o u"),
+                )
+
+        def turn_e(i, pair):
+            words = e[i][:].bitcast(F32)
+            bank = ps_turn.tile([P, 4, P], F32, tag="turn")
+            for t in range(4):
+                w0 = (4 * pair + t) * P
+                nc.tensor.transpose(bank[:, t, :], words[:, w0:w0 + P], ident_f32[:])
+            nc.scalar.copy(
+                out=e_grouped[i][:].bitcast(F32).rearrange("p (g n u) -> p g n u", g=NG, u=2)[
+                    :, 2 * pair:2 * pair + 2, :, :
+                ],
+                in_=bank[:].rearrange("p (g u) n -> p g n u", u=2),
+            )
+
+        def turn_inv_sum(i):
+            bank = ps_turn.tile([P, P], F32, tag="turn")
+            nc.tensor.transpose(bank[:], spread[i][:], ident_f32[:])
+            inv_sum[i] = three.tile([P, P], F32, name="inv_sum")
+            nc.scalar.copy(out=inv_sum[i][:], in_=bank[:])
+
+        def distances(i, h):
+            cols = slice(h * HALF, (h + 1) * HALF)
+            far_v[i, h] = two.tile([P, HALF], BF16, name="far_v")
+            nc.scalar.activation(
+                out=far_v[i, h][:], in_=right[:, cols, 1], func=ACT.Abs,
+                bias=shift_v[:, i:i + 1], scale=V_STRETCH,
+            )
+            far_u[i, h] = two.tile([P, HALF], BF16, name="far_u")
+            nc.scalar.activation(
+                out=far_u[i, h][:], in_=right[:, cols, 0], func=ACT.Abs,
+                bias=shift_u[:, i:i + 1], scale=1.0,
+            )
+
+        def caps(i, h):
+            if h == 0:
+                cap[i] = two.tile([P, N_K], BF16, name="cap")
+            cols = slice(h * HALF, (h + 1) * HALF)
+            nc.vector.tensor_tensor(
+                out=cap[i][:, cols], in0=far_v[i, h][:], in1=far_u[i, h][:], op=ALU.max
+            )
+            nc.vector.tensor_scalar(
+                out=cap[i][:, cols], in0=cap[i][:, cols], scalar1=REACH, scalar2=0.5,
+                op0=ALU.is_lt, op1=ALU.subtract,
+            )
+
+        def scores(i, j, pieces):
+            if j == 0:
+                y[i] = two.tile([P, N_K], F32, name="y")
+                chunk_max[i] = two.tile([P, NJ], F32, name="chunk_max")
+            cols = slice(j * BANK, (j + 1) * BANK)
+            bank = ps_score.tile([P, BANK], F32, tag="score")
+            gap = CB // max(len(pieces), 1)
+            for cb in range(CB):
+                nc.tensor.matmul(
+                    out=bank[:], lhsT=qT[i][:, cb, :], rhs=kT[:, cb, cols],
+                    start=(cb == 0), stop=(cb == CB - 1),
+                )
+                if cb % gap == 0 and cb // gap < len(pieces):
+                    pieces[cb // gap]()
+            score_bank[i, j] = bank
+
+        def masked(i, j):
+            cols = slice(j * BANK, (j + 1) * BANK)
+            nc.vector.scalar_tensor_tensor(
+                out=y[i][:, cols], in0=score_bank[i, j][:], scalar=SHRINK, in1=cap[i][:, cols],
+                op0=ALU.mult, op1=ALU.min,
+            )
+            nc.vector.tensor_reduce(
+                out=chunk_max[i][:, j:j + 1], in_=y[i][:, cols], axis=AXIS.X, op=ALU.max
+            )
+
+        def row_max(i):
+            top = two.tile([P, 1], F32, name="top")
+            nc.vector.tensor_reduce(out=top[:], in_=chunk_max[i][:], axis=AXIS.X, op=ALU.max)
+            exp_bias[i] = two.tile([P, 1], F32, name="exp_bias")
+            nc.vector.tensor_scalar(
+                out=exp_bias[i][:], in0=top[:], scalar1=-GROW, scalar2=None, op0=ALU.mult
+            )
+
+        def exponentials(i):
+            e[i] = two.tile([P, N_K], BF16, name="e")
+            half_sum[i] = two.tile([P, 2], F32, name="half_sum")
+            for h in range(2):
+                cols = slice(h * HALF, (h + 1) * HALF)
+                nc.scalar.activation(
+                    out=e[i][:, cols], in_=y[i][:, cols], func=ACT.Exp,
+                    bias=exp_bias[i][:, 0:1], scale=GROW, accum_out=half_sum[i][:, h:h + 1],
+                )
+            e_grouped[i] = two.tile([P, N_K], BF16, name="e_grouped", align_bytes=64)
+
+        def normaliser(i):
+            total = two.tile([P, 1], F32, name="total")
+            nc.vector.tensor_reduce(out=total[:], in_=half_sum[i][:], axis=AXIS.X, op=ALU.add)
+            inverse = two.tile([P, 1], F32, name="inverse")
+            nc.vector.reciprocal(out=inverse[:], in_=total[:])
+            spread[i] = two.tile([P, P], F32, name="spread")
+            nc.vector.tensor_scalar(
+                out=spread[i][:], in0=ones[:], scalar1=inverse[:, 0:1], scalar2=None, op0=ALU.mult
+            )
+
+        def quantise_e(i):
+            e_codes[i] = three.tile([P, NG * P], U32, name="e_codes", align_bytes=64)
+            e_scales[i] = three.tile([P, NG * P], U8, name="e_scales", align_bytes=64)
+            nc.vector.quantize_mx(
+                out=e_codes[i][:].bitcast(FP8X4), scales=e_scales[i][:], in_=e_grouped[i][:]
+            )
+
+        def group_values(g):
+            v_grouped[g] = two.tile([P, C, 4], BF16, name="v_grouped", tag="grouped", align_bytes=64)
+            nc.vector.tensor_copy(
+                out=v_grouped[g][:].rearrange("p (a e q) t -> p a e q t", a=4, e=2),
+                in_=v_raw[g][:].rearrange("p t (a q e) -> p a e q t", a=4, e=2),
+            )
+
+        def quantise_values(g):
+            nc.vector.quantize_mx(
+                out=v_codes[:, g, :].bitcast(FP8X4), scales=v_scales[:, g, :],
+                in_=v_grouped[g][:].rearrange("p c t -> p (c t)"),
+            )
+
+        def quantise_weights():
+            for f in range(NF):
+                nc.vector.quantize_mx(
+                    out=w_codes[:, f, :].bitcast(FP8X4), scales=w_scales[:, f, :],
+                    in_=w_grouped[f][:],
+                )
+
+        def attend(i):
+            m_grouped[i] = two.tile([P, NF, P, 4], BF16, name="m_grouped", align_bytes=64)
+            for f in range(NF):
+                bank = ps_mx.tile([P, 4, P], F32, tag="mx")
+                for t in range(4):
+                    c0 = (4 * f + t) * P
+                    for g in range(NG):
+                        nc.tensor.matmul_mx(
+                            out=bank[:, t, :],
+                            lhsT=v_codes[:, g, c0:c0 + P].bitcast(FP8X4),
+                            lhsT_scale=v_scales[:, g, c0:c0 + P],
+                            rhs=e_codes[i][:, g * P:(g + 1) * P].bitcast(FP8X4),
+                            rhs_scale=e_scales[i][:, g * P:(g + 1) * P],
+                            start=(g == 0), stop=(g == NG - 1),
+                        )
+                nc.vector.tensor_tensor(
+                    out=m_grouped[i][:, f, :, :],
+                    in0=bank[:].rearrange("p t n -> p n t"),
+                    in1=inv_sum[i][:].unsqueeze(2).to_broadcast([P, P, 4]),
+                    op=ALU.mult,
+                )
+
+        def quantise_matched(i):
+            m_codes[i] = two.tile([P, NF * P], U32, name="m_codes", align_bytes=64)
+            m_scales[i] = two.tile([P, NF * P], U8, name="m_scales", align_bytes=64)
+            nc.vector.quantize_mx(
+                out=m_codes[i][:].bitcast(FP8X4), scales=m_scales[i][:],
+                in_=m_grouped[i][:].rearrange("p f n t -> p (f n t)"),
+            )
+
+        def project(i):
+            result = two.tile([P, C], F32, name="result")
+            for h in range(C // BANK):
+                cols = slice(h * BANK, (h + 1) * BANK)
+                bank = ps_mx.tile([P, BANK], F32, tag="mx")
+                for f in range(NF):
+                    nc.tensor.matmul_mx(
+                        out=bank[:],
+                        lhsT=m_codes[i][:, f * P:(f + 1) * P].bitcast(FP8X4),
+                        lhsT_scale=m_scales[i][:, f * P:(f + 1) * P],
+                        rhs=w_codes[:, f, cols].bitcast(FP8X4),
+                        rhs_scale=w_scales[:, f, cols],
+                        start=(f == 0), stop=(f == NF - 1),
+                    )
+                nc.vector.tensor_tensor(
+                    out=result[:, cols], in0=bank[:], in1=bias[:, cols], op=ALU.add
+                )
+            nc.sync.dma_start(out=out_rows[i], in_=result[:])
+
+        def key_pieces(j):
+            return [lambda piece=piece: turn_keys(j, piece) for piece in range(8)]
+
+        def query_pieces(i):
+            return [lambda half=half: turn_queries(i, half) for half in range(2)]
+
+        def weight_pieces(first):
+            return [lambda b=b: turn_weights(b) for b in range(first, first + 2)]
+
+        def e_pieces(i):
+            return [lambda: turn_e(i, 0), lambda: turn_e(i, 1), lambda: turn_inv_sum(i)]
+
+        for piece in query_pieces(0) + key_pieces(0):
+            piece()
+        distances(0, 0)
+        distances(0, 1)
+
+        for i in range(NT):
+            first = i == 0
+            more = i + 1 < NT
+            if i == 2:
+                for f in range(NF):
+                    w_grouped[f] = two.tile([P, 4 * C], BF16, name="w_grouped", align_bytes=64)
+            extra = [weight_pieces(2 * j) if i == 2 else [] for j in range(NJ)]
+            if i >= 1:
+                exponentials(i - 1)
+            scores(i, 0, (key_pieces(1) if first else []) + extra[0])
+            if first:
+                caps(0, 0)
+            masked(i, 0)
+            if i == LAG:
+                quantise_values(3)
+            if i >= LAG:
+                attend(i - LAG)
+            if i >= 1:
+                normaliser(i - 1)
+            if i >= LAG:
+                quantise_matched(i - LAG)
+            scores(i, 1, (key_pieces(2) if first else []) + extra[1])
+            masked(i, 1)
+            if first:
+                caps(0, 1)
+            if i == 1:
+                group_values(0)
+            if i == 2:
+                group_values(2)
+                quantise_values(1)
+            if i == LAG:
+                quantise_weights()
+            if more:
+                distances(i + 1, 0)
+                distances(i + 1, 1)
+            scores(i, 2, (key_pieces(3) if first else e_pieces(i - 1)) + extra[2])
+            masked(i, 2)
+            if i >= LAG:
+                project(i - LAG)
+            if more:
+                caps(i + 1, 0)
+            if i >= 1:
+                quantise_e(i - 1)
+            scores(i, 3, (query_pieces(i + 1) if more else []) + extra[3])
+            if more:
+                caps(i + 1, 1)
+            masked(i, 3)
+            row_max(i)
+            if i == 1:
+                group_values(1)
+                quantise_values(0)
+            if i == 2:
+                group_values(3)
+                quantise_values(2)
+
+        last = NT - 1
+        exponentials(last)
+        attend(last - 2)
+        quantise_matched(last - 2)
+        attend(last - 1)
+        quantise_matched(last - 1)
+        normaliser(last)
+        for piece in e_pieces(last):
+            piece()
+        project(last - 2)
+        project(last - 1)
+        quantise_e(last)
+        attend(last)
+        quantise_matched(last)
+        project(last)

@@ -47,7 +47,6 @@ def tile_epipolarcrossattention_pa_kernel(tc, Q, K, V, kpts_L, kpts_R, Wm, bm, o
         ps_score = ctx.enter_context(tc.psum_pool(name="ps_score", bufs=2))
         ps_turn = ctx.enter_context(tc.psum_pool(name="ps_turn", bufs=3))
         ps_mx = ctx.enter_context(tc.psum_pool(name="ps_mx", bufs=3))
-        ctx.enter_context(tc.manual_schedule())
 
         q_rows = Q.rearrange("(p i) c -> i p c", i=NT)
         out_rows = out.rearrange("(p i) o -> i p o", i=NT)

@@ -17,7 +17,7 @@ N_Q = 1024
 N_K = 2048
 C = 1024
 NT = N_Q // P
-CB = C // P
+NW = C // (2 * P)
 BANK = 512
 NJ = N_K // BANK
 K_PASS = 512
@@ -91,8 +91,6 @@ def tile_epipolarcrossattention_pa_kernel(tc, Q, K, V, kpts_L, kpts_R, Wm, bm, o
         for i in range(3, NT):
             load_queries(i)
 
-        ident_bf = keep.tile([P, P], BF16)
-        make_identity(nc, ident_bf[:])
         ident_f32 = keep.tile([P, P], F32)
         make_identity(nc, ident_f32[:])
         ones = keep.tile([P, P], F32)
@@ -107,7 +105,7 @@ def tile_epipolarcrossattention_pa_kernel(tc, Q, K, V, kpts_L, kpts_R, Wm, bm, o
             op0=ALU.mult, op1=ALU.add,
         )
 
-        kT = keep.tile([P, CB, N_K], BF16)
+        kT = keep.tile([P, NW, N_K, 2], BF16)
         v_codes = keep.tile([P, NG, C], U32, align_bytes=64)
         v_scales = keep.tile([P, NG, C], U8, align_bytes=64)
         w_codes = keep.tile([P, NF, C], U32, align_bytes=64)
@@ -134,23 +132,23 @@ def tile_epipolarcrossattention_pa_kernel(tc, Q, K, V, kpts_L, kpts_R, Wm, bm, o
         v_grouped = {}
         score_bank = {}
 
-        def turn_keys(j, piece):
-            b, half = piece // 2, piece % 2
-            bank = ps_turn.tile([P, 4, P], BF16, tag="turn")
-            for t in range(4):
-                cb = 4 * half + t
-                nc.tensor.transpose(bank[:, t, :], k_raw[j][:, b, cb * P:(cb + 1) * P], ident_bf[:])
-            dst = kT[:, 4 * half:4 * half + 4, j * BANK + b * P:j * BANK + (b + 1) * P]
-            nc.vector.tensor_copy(out=dst, in_=bank[:])
+        def turn_keys(j, b):
+            words = k_raw[j][:, b, :].bitcast(F32)
+            bank = ps_turn.tile([P, NW, P], F32, tag="turn")
+            for w in range(NW):
+                nc.tensor.transpose(bank[:, w, :], words[:, w * P:(w + 1) * P], ident_f32[:])
+            m0 = j * BANK + b * P
+            nc.vector.tensor_copy(
+                out=kT[:].rearrange("p w m e -> p w (m e)").bitcast(F32)[:, :, m0:m0 + P], in_=bank[:]
+            )
 
-        def turn_queries(i, half):
-            if half == 0:
-                qT[i] = two.tile([P, CB, P], BF16, name="qT")
-            bank = ps_turn.tile([P, 4, P], BF16, tag="turn")
-            for t in range(4):
-                cb = 4 * half + t
-                nc.tensor.transpose(bank[:, t, :], q_raw[i][:, cb * P:(cb + 1) * P], ident_bf[:])
-            nc.scalar.copy(out=qT[i][:, 4 * half:4 * half + 4, :], in_=bank[:])
+        def turn_queries(i):
+            qT[i] = two.tile([P, NW, P, 2], BF16, name="qT")
+            words = q_raw[i][:].bitcast(F32)
+            bank = ps_turn.tile([P, NW, P], F32, tag="turn")
+            for w in range(NW):
+                nc.tensor.transpose(bank[:, w, :], words[:, w * P:(w + 1) * P], ident_f32[:])
+            nc.scalar.copy(out=qT[i][:].rearrange("p w n e -> p w (n e)").bitcast(F32), in_=bank[:])
 
         def turn_weights(b):
             words = w_raw[b // 4][:, b % 4, :].bitcast(F32)
@@ -215,14 +213,16 @@ def tile_epipolarcrossattention_pa_kernel(tc, Q, K, V, kpts_L, kpts_R, Wm, bm, o
                 chunk_max[i] = two.tile([P, NJ], F32, name="chunk_max")
             cols = slice(j * BANK, (j + 1) * BANK)
             bank = ps_score.tile([P, BANK], F32, tag="score")
-            gap = CB // max(len(pieces), 1)
-            for cb in range(CB):
+            passes = 2 * NW
+            gap = passes // max(len(pieces), 1)
+            for k in range(passes):
+                w, e01 = k // 2, k % 2
                 nc.tensor.matmul(
-                    out=bank[:], lhsT=qT[i][:, cb, :], rhs=kT[:, cb, cols],
-                    start=(cb == 0), stop=(cb == CB - 1),
+                    out=bank[:], lhsT=qT[i][:, w, :, e01], rhs=kT[:, w, cols, e01],
+                    start=(k == 0), stop=(k == passes - 1),
                 )
-                if cb % gap == 0 and cb // gap < len(pieces):
-                    pieces[cb // gap]()
+                if k % gap == 0 and k // gap < len(pieces):
+                    pieces[k // gap]()
             score_bank[i, j] = bank
 
         def masked(i, j):
@@ -273,10 +273,13 @@ def tile_epipolarcrossattention_pa_kernel(tc, Q, K, V, kpts_L, kpts_R, Wm, bm, o
 
         def group_values(g):
             v_grouped[g] = two.tile([P, C, 4], BF16, name="v_grouped", tag="grouped", align_bytes=64)
-            nc.vector.tensor_copy(
-                out=v_grouped[g][:].rearrange("p (a e q) t -> p a e q t", a=4, e=2),
-                in_=v_raw[g][:].rearrange("p t (a q e) -> p a e q t", a=4, e=2),
-            )
+            dst = v_grouped[g][:].rearrange("p (a e q) t -> p a e q t", a=4, e=2)
+            src = v_raw[g][:].rearrange("p t (a q e) -> p a e q t", a=4, e=2)
+            for a in range(4):
+                nc.gpsimd.tensor_scalar(
+                    out=dst[:, a], in0=src[:, a], scalar1=1.0, scalar2=0.0,
+                    op0=ALU.mult, op1=ALU.add,
+                )
 
         def quantise_values(g):
             nc.vector.quantize_mx(
@@ -338,13 +341,13 @@ def tile_epipolarcrossattention_pa_kernel(tc, Q, K, V, kpts_L, kpts_R, Wm, bm, o
                 nc.vector.tensor_tensor(
                     out=result[:, cols], in0=bank[:], in1=bias[:, cols], op=ALU.add
                 )
-            nc.sync.dma_start(out=out_rows[i], in_=result[:])
+                nc.sync.dma_start(out=out_rows[i][:, cols], in_=result[:, cols])
 
         def key_pieces(j):
-            return [lambda piece=piece: turn_keys(j, piece) for piece in range(8)]
+            return [lambda b=b: turn_keys(j, b) for b in range(4)]
 
         def query_pieces(i):
-            return [lambda half=half: turn_queries(i, half) for half in range(2)]
+            return [lambda: turn_queries(i)]
 
         def weight_pieces(first):
             return [lambda b=b: turn_weights(b) for b in range(first, first + 2)]

@@ -17,14 +17,13 @@ N_Q = 1024
 N_K = 2048
 C = 1024
 NT = N_Q // P
-NW = C // (2 * P)
+CB = C // P
 BANK = 512
 NJ = N_K // BANK
 K_PASS = 512
 NG = N_K // K_PASS
 NF = C // K_PASS
 HALF = N_K // 2
-LAG = 3
 
 FLOPS = 2 * N_Q * N_K * C + 2 * N_Q * N_K * C + 2 * N_Q * C * C
 
@@ -42,11 +41,10 @@ def tile_epipolarcrossattention_pa_kernel(tc, Q, K, V, kpts_L, kpts_R, Wm, bm, o
         keep = ctx.enter_context(tc.tile_pool(name="keep", bufs=1))
         raw = ctx.enter_context(tc.tile_pool(name="raw", bufs=5))
         q_in = ctx.enter_context(tc.tile_pool(name="q_in", bufs=3))
+        one = ctx.enter_context(tc.tile_pool(name="one", bufs=1))
         two = ctx.enter_context(tc.tile_pool(name="two", bufs=2))
-        three = ctx.enter_context(tc.tile_pool(name="three", bufs=3))
-        ps_score = ctx.enter_context(tc.psum_pool(name="ps_score", bufs=2))
-        ps_turn = ctx.enter_context(tc.psum_pool(name="ps_turn", bufs=3))
-        ps_mx = ctx.enter_context(tc.psum_pool(name="ps_mx", bufs=3))
+        ps_turn = ctx.enter_context(tc.psum_pool(name="ps_turn", bufs=4))
+        ctx.enter_context(tc.manual_schedule())
 
         q_rows = Q.rearrange("(p i) c -> i p c", i=NT)
         out_rows = out.rearrange("(p i) o -> i p o", i=NT)
@@ -63,6 +61,12 @@ def tile_epipolarcrossattention_pa_kernel(tc, Q, K, V, kpts_L, kpts_R, Wm, bm, o
             q_raw[i] = q_in.tile([P, C], BF16, name="q_raw")
             nc.sync.dma_start(out=q_raw[i][:], in_=q_rows[i])
 
+        def load_values(g):
+            v_raw[g] = raw.tile([P, 4, C], BF16, name="v_raw", tag="raw")
+            nc.sync.dma_start(
+                out=v_raw[g][:].rearrange("p (u e) c -> p u e c", u=2), in_=v_rows[g]
+            )
+
         left = keep.tile([P, NT, 2], BF16)
         nc.sync.dma_start(out=left[:], in_=kpts_L.rearrange("(p i) c -> p i c", i=NT))
         load_queries(0)
@@ -77,20 +81,20 @@ def tile_epipolarcrossattention_pa_kernel(tc, Q, K, V, kpts_L, kpts_R, Wm, bm, o
                     in_=kpts_R.rearrange("m c -> (m c)").partition_broadcast(P),
                 )
         load_queries(1)
-        for g in range(NG):
-            v_raw[g] = raw.tile([P, 4, C], BF16, name="v_raw", tag="raw")
-            nc.sync.dma_start(
-                out=v_raw[g][:].rearrange("p (u e) c -> p u e c", u=2), in_=v_rows[g]
-            )
-        load_queries(2)
         for h in range(2):
             w_raw[h] = raw.tile([P, 4, C], BF16, name="w_raw", tag="raw")
             nc.sync.dma_start(out=w_raw[h][:], in_=w_rows[h])
-        bias = keep.tile([P, C], BF16)
-        nc.sync.dma_start(out=bias[:], in_=bm.partition_broadcast(P))
+        load_queries(2)
+        for g in range(NG - 1):
+            load_values(g)
         for i in range(3, NT):
             load_queries(i)
+        load_values(NG - 1)
+        bias = keep.tile([P, C], BF16)
+        nc.sync.dma_start(out=bias[:], in_=bm.partition_broadcast(P))
 
+        ident_bf = keep.tile([P, P], BF16)
+        make_identity(nc, ident_bf[:])
         ident_f32 = keep.tile([P, P], F32)
         make_identity(nc, ident_f32[:])
         ones = keep.tile([P, P], F32)
@@ -105,11 +109,14 @@ def tile_epipolarcrossattention_pa_kernel(tc, Q, K, V, kpts_L, kpts_R, Wm, bm, o
             op0=ALU.mult, op1=ALU.add,
         )
 
-        kT = keep.tile([P, NW, N_K, 2], BF16)
+        kT = keep.tile([P, CB, N_K], BF16)
         v_codes = keep.tile([P, NG, C], U32, align_bytes=64)
         v_scales = keep.tile([P, NG, C], U8, align_bytes=64)
         w_codes = keep.tile([P, NF, C], U32, align_bytes=64)
         w_scales = keep.tile([P, NF, C], U8, align_bytes=64)
+        e_codes = keep.tile([P, NT, NG * P], U32, align_bytes=64)
+        e_scales = keep.tile([P, NT, NG * P], U8, align_bytes=64)
+        inv_sum = keep.tile([P, NT, P], F32)
 
         qT = {}
         far_v = {}
@@ -122,9 +129,6 @@ def tile_epipolarcrossattention_pa_kernel(tc, Q, K, V, kpts_L, kpts_R, Wm, bm, o
         half_sum = {}
         spread = {}
         e_grouped = {}
-        e_codes = {}
-        e_scales = {}
-        inv_sum = {}
         m_grouped = {}
         m_codes = {}
         m_scales = {}
@@ -132,55 +136,74 @@ def tile_epipolarcrossattention_pa_kernel(tc, Q, K, V, kpts_L, kpts_R, Wm, bm, o
         v_grouped = {}
         score_bank = {}
 
-        def turn_keys(j, b):
-            words = k_raw[j][:, b, :].bitcast(F32)
-            bank = ps_turn.tile([P, NW, P], F32, tag="turn")
-            for w in range(NW):
-                nc.tensor.transpose(bank[:, w, :], words[:, w * P:(w + 1) * P], ident_f32[:])
-            m0 = j * BANK + b * P
-            nc.vector.tensor_copy(
-                out=kT[:].rearrange("p w m e -> p w (m e)").bitcast(F32)[:, :, m0:m0 + P], in_=bank[:]
-            )
+        def turning(sources, identity, per_step, leave):
+            held = {}
+
+            def step(s):
+                if s == 0:
+                    held[0] = ps_turn.tile(
+                        [P, len(sources), P], identity.dtype, name="turned", tag="turn"
+                    )
+                for t in range(s * per_step, (s + 1) * per_step):
+                    nc.tensor.transpose(held[0][:, t, :], sources[t], identity)
+                if (s + 1) * per_step == len(sources):
+                    leave(held[0])
+
+            return [lambda s=s: step(s) for s in range(len(sources) // per_step)]
+
+        def turn_keys(j):
+            steps = []
+            for b in range(4):
+                m0 = j * BANK + b * P
+                steps.extend(turning(
+                    [k_raw[j][:, b, cb * P:(cb + 1) * P] for cb in range(CB)], ident_bf[:], 4,
+                    lambda bank, m0=m0: nc.vector.tensor_copy(out=kT[:, :, m0:m0 + P], in_=bank[:]),
+                ))
+            return steps
 
         def turn_queries(i):
-            qT[i] = two.tile([P, NW, P, 2], BF16, name="qT")
-            words = q_raw[i][:].bitcast(F32)
-            bank = ps_turn.tile([P, NW, P], F32, tag="turn")
-            for w in range(NW):
-                nc.tensor.transpose(bank[:, w, :], words[:, w * P:(w + 1) * P], ident_f32[:])
-            nc.scalar.copy(out=qT[i][:].rearrange("p w n e -> p w (n e)").bitcast(F32), in_=bank[:])
-
-        def turn_weights(b):
-            words = w_raw[b // 4][:, b % 4, :].bitcast(F32)
-            bank = ps_turn.tile([P, 4, P], F32, tag="turn")
-            for t in range(4):
-                nc.tensor.transpose(bank[:, t, :], words[:, t * P:(t + 1) * P], ident_f32[:])
-            for f in range(NF):
-                nc.scalar.copy(
-                    out=w_grouped[f][:].bitcast(F32).rearrange("p (o u) -> p o u", u=2)[
-                        :, b * P:(b + 1) * P, :
-                    ],
-                    in_=bank[:, 2 * f:2 * f + 2, :].rearrange("p u o -> p o u"),
-                )
-
-        def turn_e(i, pair):
-            words = e[i][:].bitcast(F32)
-            bank = ps_turn.tile([P, 4, P], F32, tag="turn")
-            for t in range(4):
-                w0 = (4 * pair + t) * P
-                nc.tensor.transpose(bank[:, t, :], words[:, w0:w0 + P], ident_f32[:])
-            nc.scalar.copy(
-                out=e_grouped[i][:].bitcast(F32).rearrange("p (g n u) -> p g n u", g=NG, u=2)[
-                    :, 2 * pair:2 * pair + 2, :, :
-                ],
-                in_=bank[:].rearrange("p (g u) n -> p g n u", u=2),
+            qT[i] = two.tile([P, CB, P], BF16, name="qT")
+            return turning(
+                [q_raw[i][:, cb * P:(cb + 1) * P] for cb in range(CB)], ident_bf[:], 2,
+                lambda bank: nc.scalar.copy(out=qT[i][:], in_=bank[:]),
             )
 
+        def turn_weights(f, pair):
+            if pair == 0:
+                w_grouped[f] = one.tile([P, 4 * C], BF16, name="w_grouped", align_bytes=64)
+            sources = []
+            for block in (2 * pair, 2 * pair + 1):
+                words = w_raw[block // 4][:, block % 4, :].bitcast(F32)
+                for u in range(2):
+                    sources.append(words[:, (2 * f + u) * P:(2 * f + u + 1) * P])
+            return turning(sources, ident_f32[:], 1, lambda bank: nc.scalar.copy(
+                out=w_grouped[f][:].bitcast(F32).rearrange("p (b o u) -> p b o u", o=P, u=2)[
+                    :, 2 * pair:2 * pair + 2, :, :
+                ],
+                in_=bank[:].rearrange("p (b u) o -> p b o u", u=2),
+            ))
+
+        def turn_e(i):
+            words = e[i][:].bitcast(F32)
+            steps = []
+            for pair in range(2):
+                steps.extend(turning(
+                    [words[:, (4 * pair + t) * P:(4 * pair + t + 1) * P] for t in range(4)],
+                    ident_f32[:], 1,
+                    lambda bank, pair=pair: nc.scalar.copy(
+                        out=e_grouped[i][:].bitcast(F32).rearrange(
+                            "p (g n u) -> p g n u", g=NG, u=2
+                        )[:, 2 * pair:2 * pair + 2, :, :],
+                        in_=bank[:].rearrange("p (g u) n -> p g n u", u=2),
+                    ),
+                ))
+            return steps
+
         def turn_inv_sum(i):
-            bank = ps_turn.tile([P, P], F32, tag="turn")
-            nc.tensor.transpose(bank[:], spread[i][:], ident_f32[:])
-            inv_sum[i] = three.tile([P, P], F32, name="inv_sum")
-            nc.scalar.copy(out=inv_sum[i][:], in_=bank[:])
+            return turning(
+                [spread[i][:]], ident_f32[:], 1,
+                lambda bank: nc.scalar.copy(out=inv_sum[:, i, :], in_=bank[:, 0, :]),
+            )
 
         def distances(i, h):
             cols = slice(h * HALF, (h + 1) * HALF)
@@ -207,25 +230,22 @@ def tile_epipolarcrossattention_pa_kernel(tc, Q, K, V, kpts_L, kpts_R, Wm, bm, o
                 op0=ALU.is_lt, op1=ALU.subtract,
             )
 
-        def scores(i, j, pieces):
-            if j == 0:
-                y[i] = two.tile([P, N_K], F32, name="y")
-                chunk_max[i] = two.tile([P, NJ], F32, name="chunk_max")
+        def scores(i, j, steps):
             cols = slice(j * BANK, (j + 1) * BANK)
             bank = ps_score.tile([P, BANK], F32, tag="score")
-            passes = 2 * NW
-            gap = passes // max(len(pieces), 1)
-            for k in range(passes):
-                w, e01 = k // 2, k % 2
+            for cb in range(CB):
                 nc.tensor.matmul(
-                    out=bank[:], lhsT=qT[i][:, w, :, e01], rhs=kT[:, w, cols, e01],
-                    start=(k == 0), stop=(k == passes - 1),
+                    out=bank[:], lhsT=qT[i][:, cb, :], rhs=kT[:, cb, cols],
+                    start=(cb == 0), stop=(cb == CB - 1),
                 )
-                if k % gap == 0 and k // gap < len(pieces):
-                    pieces[k // gap]()
+                if cb < len(steps):
+                    steps[cb]()
             score_bank[i, j] = bank
 
         def masked(i, j):
+            if j == 0:
+                y[i] = two.tile([P, N_K], F32, name="y")
+                chunk_max[i] = two.tile([P, NJ], F32, name="chunk_max")
             cols = slice(j * BANK, (j + 1) * BANK)
             nc.vector.scalar_tensor_tensor(
                 out=y[i][:, cols], in0=score_bank[i, j][:], scalar=SHRINK, in1=cap[i][:, cols],
@@ -265,21 +285,17 @@ def tile_epipolarcrossattention_pa_kernel(tc, Q, K, V, kpts_L, kpts_R, Wm, bm, o
             )
 
         def quantise_e(i):
-            e_codes[i] = three.tile([P, NG * P], U32, name="e_codes", align_bytes=64)
-            e_scales[i] = three.tile([P, NG * P], U8, name="e_scales", align_bytes=64)
             nc.vector.quantize_mx(
-                out=e_codes[i][:].bitcast(FP8X4), scales=e_scales[i][:], in_=e_grouped[i][:]
+                out=e_codes[:, i, :].bitcast(FP8X4), scales=e_scales[:, i, :], in_=e_grouped[i][:]
             )
 
-        def group_values(g):
-            v_grouped[g] = two.tile([P, C, 4], BF16, name="v_grouped", tag="grouped", align_bytes=64)
-            dst = v_grouped[g][:].rearrange("p (a e q) t -> p a e q t", a=4, e=2)
-            src = v_raw[g][:].rearrange("p t (a q e) -> p a e q t", a=4, e=2)
-            for a in range(4):
-                nc.gpsimd.tensor_scalar(
-                    out=dst[:, a], in0=src[:, a], scalar1=1.0, scalar2=0.0,
-                    op0=ALU.mult, op1=ALU.add,
-                )
+        def group_values(g, a):
+            if a == 0:
+                v_grouped[g] = one.tile([P, C, 4], BF16, name="v_grouped", align_bytes=64)
+            nc.vector.tensor_copy(
+                out=v_grouped[g][:].rearrange("p (a e q) t -> p a e q t", a=4, e=2)[:, a],
+                in_=v_raw[g][:].rearrange("p t (a q e) -> p a e q t", a=4, e=2)[:, a],
+            )
 
         def quantise_values(g):
             nc.vector.quantize_mx(
@@ -287,12 +303,10 @@ def tile_epipolarcrossattention_pa_kernel(tc, Q, K, V, kpts_L, kpts_R, Wm, bm, o
                 in_=v_grouped[g][:].rearrange("p c t -> p (c t)"),
             )
 
-        def quantise_weights():
-            for f in range(NF):
-                nc.vector.quantize_mx(
-                    out=w_codes[:, f, :].bitcast(FP8X4), scales=w_scales[:, f, :],
-                    in_=w_grouped[f][:],
-                )
+        def quantise_weights(f):
+            nc.vector.quantize_mx(
+                out=w_codes[:, f, :].bitcast(FP8X4), scales=w_scales[:, f, :], in_=w_grouped[f][:]
+            )
 
         def attend(i):
             m_grouped[i] = two.tile([P, NF, P, 4], BF16, name="m_grouped", align_bytes=64)
@@ -305,14 +319,14 @@ def tile_epipolarcrossattention_pa_kernel(tc, Q, K, V, kpts_L, kpts_R, Wm, bm, o
                             out=bank[:, t, :],
                             lhsT=v_codes[:, g, c0:c0 + P].bitcast(FP8X4),
                             lhsT_scale=v_scales[:, g, c0:c0 + P],
-                            rhs=e_codes[i][:, g * P:(g + 1) * P].bitcast(FP8X4),
-                            rhs_scale=e_scales[i][:, g * P:(g + 1) * P],
+                            rhs=e_codes[:, i, g * P:(g + 1) * P].bitcast(FP8X4),
+                            rhs_scale=e_scales[:, i, g * P:(g + 1) * P],
                             start=(g == 0), stop=(g == NG - 1),
                         )
                 nc.vector.tensor_tensor(
                     out=m_grouped[i][:, f, :, :],
                     in0=bank[:].rearrange("p t n -> p n t"),
-                    in1=inv_sum[i][:].unsqueeze(2).to_broadcast([P, P, 4]),
+                    in1=inv_sum[:, i, :].unsqueeze(2).to_broadcast([P, P, 4]),
                     op=ALU.mult,
                 )
 
@@ -343,90 +357,95 @@ def tile_epipolarcrossattention_pa_kernel(tc, Q, K, V, kpts_L, kpts_R, Wm, bm, o
                 )
                 nc.sync.dma_start(out=out_rows[i][:, cols], in_=result[:, cols])
 
-        def key_pieces(j):
-            return [lambda b=b: turn_keys(j, b) for b in range(4)]
+        def run(steps):
+            for step in steps:
+                step()
 
-        def query_pieces(i):
-            return [lambda: turn_queries(i)]
+        background = []
+        for g in range(NG):
+            background.extend([lambda g=g, a=a: group_values(g, a) for a in range(4)])
+            background.append(lambda g=g: quantise_values(g))
 
-        def weight_pieces(first):
-            return [lambda b=b: turn_weights(b) for b in range(first, first + 2)]
+        def fill(i, j):
+            item = NJ * (i - 1) + j
+            if 0 <= item < len(background):
+                background[item]()
 
-        def e_pieces(i):
-            return [lambda: turn_e(i, 0), lambda: turn_e(i, 1), lambda: turn_inv_sum(i)]
-
-        for piece in query_pieces(0) + key_pieces(0):
-            piece()
-        distances(0, 0)
-        distances(0, 1)
-
-        for i in range(NT):
-            first = i == 0
+        def softmax_round(i):
+            live = i < NT
             more = i + 1 < NT
-            if i == 2:
-                for f in range(NF):
-                    w_grouped[f] = two.tile([P, 4 * C], BF16, name="w_grouped", align_bytes=64)
-            extra = [weight_pieces(2 * j) if i == 2 else [] for j in range(NJ)]
-            if i >= 1:
-                exponentials(i - 1)
-            scores(i, 0, (key_pieces(1) if first else []) + extra[0])
-            if first:
-                caps(0, 0)
-            masked(i, 0)
-            if i == LAG:
-                quantise_values(3)
-            if i >= LAG:
-                attend(i - LAG)
-            if i >= 1:
-                normaliser(i - 1)
-            if i >= LAG:
-                quantise_matched(i - LAG)
-            scores(i, 1, (key_pieces(2) if first else []) + extra[1])
-            masked(i, 1)
-            if first:
-                caps(0, 1)
-            if i == 1:
-                group_values(0)
-            if i == 2:
-                group_values(2)
-                quantise_values(1)
-            if i == LAG:
-                quantise_weights()
+            steps = [[], [], [], []]
+            if i == 0:
+                steps = [turn_keys(1), turn_keys(2), turn_keys(3), []]
+            if 2 <= i:
+                steps[0] = turn_e(i - 2)
+            if 2 <= i and live:
+                normaliser(i - 2)
+                steps[3] = turn_inv_sum(i - 2)
             if more:
                 distances(i + 1, 0)
-                distances(i + 1, 1)
-            scores(i, 2, (key_pieces(3) if first else e_pieces(i - 1)) + extra[2])
-            masked(i, 2)
-            if i >= LAG:
-                project(i - LAG)
+            if live:
+                scores(i, 0, steps[0])
+            else:
+                run(steps[0])
+            if 1 <= i <= NT:
+                exponentials(i - 1)
+            if i == 0:
+                caps(0, 0)
+            if live:
+                masked(i, 0)
+            if 2 <= i:
+                quantise_e(i - 2)
+            fill(i, 0)
+            if live:
+                scores(i, 1, steps[1] if i == 0 else steps[1] + (turn_queries(i + 1) if more else []))
+            else:
+                run(steps[1])
             if more:
                 caps(i + 1, 0)
-            if i >= 1:
-                quantise_e(i - 1)
-            scores(i, 3, (query_pieces(i + 1) if more else []) + extra[3])
+            if i == 0:
+                caps(0, 1)
+            if live:
+                masked(i, 1)
+            fill(i, 1)
+            if more:
+                distances(i + 1, 1)
+            if 1 <= i <= 2 * NF:
+                f, half = (i - 1) // 2, (i - 1) % 2
+                steps[2] = turn_weights(f, 2 * half) + turn_weights(f, 2 * half + 1)
+            if live:
+                scores(i, 2, steps[2])
+                masked(i, 2)
+            fill(i, 2)
+            if i == 0:
+                steps[3] = turn_queries(1)
+            if live:
+                scores(i, 3, steps[3])
+                masked(i, 3)
+                row_max(i)
             if more:
                 caps(i + 1, 1)
-            masked(i, 3)
-            row_max(i)
-            if i == 1:
-                group_values(1)
-                quantise_values(0)
-            if i == 2:
-                group_values(3)
-                quantise_values(2)
+            if 1 <= i <= 2 * NF and (i - 1) % 2 == 1:
+                quantise_weights((i - 1) // 2)
+            fill(i, 3)
 
-        last = NT - 1
-        exponentials(last)
-        attend(last - 2)
-        quantise_matched(last - 2)
-        attend(last - 1)
-        quantise_matched(last - 1)
-        normaliser(last)
-        for piece in e_pieces(last):
-            piece()
-        project(last - 2)
-        project(last - 1)
-        quantise_e(last)
-        attend(last)
-        quantise_matched(last)
-        project(last)
+        run(turn_queries(0) + turn_keys(0))
+        distances(0, 0)
+        distances(0, 1)
+        with tc.psum_pool(name="ps_score", bufs=4) as ps_score:
+            for i in range(NT + 1):
+                softmax_round(i)
+
+        with tc.psum_pool(name="ps_mx", bufs=4, reuse_waits="tile") as ps_mx:
+            for i in range(NT + 1):
+                if i == 2:
+                    normaliser(NT - 2)
+                    normaliser(NT - 1)
+                if i == 3:
+                    softmax_round(NT + 1)
+                    run(turn_inv_sum(NT - 2) + turn_inv_sum(NT - 1))
+                if i < NT:
+                    attend(i)
+                    quantise_matched(i)
+                if i >= 1:
+                    project(i - 1)

@@ -31,8 +31,8 @@ V_TOL = 3.0
 MAX_DISP = 192.0
 REACH = MAX_DISP / 2.0
 V_STRETCH = REACH / V_TOL
-SHRINK = 2.0 ** -40
-GROW = 2.0 ** 35
+SHRINK = 2.0 ** -72
+GROW = 2.0 ** 67
 
 
 def tile_epipolarcrossattention_pa_kernel(tc, Q, K, V, kpts_L, kpts_R, Wm, bm, out):
@@ -93,8 +93,6 @@ def tile_epipolarcrossattention_pa_kernel(tc, Q, K, V, kpts_L, kpts_R, Wm, bm, o
         bias = keep.tile([P, C], BF16)
         nc.sync.dma_start(out=bias[:], in_=bm.partition_broadcast(P))
 
-        ident_bf = keep.tile([P, P], BF16)
-        make_identity(nc, ident_bf[:])
         ident_f32 = keep.tile([P, P], F32)
         make_identity(nc, ident_f32[:])
         ones = keep.tile([P, P], F32)
@@ -109,7 +107,7 @@ def tile_epipolarcrossattention_pa_kernel(tc, Q, K, V, kpts_L, kpts_R, Wm, bm, o
             op0=ALU.mult, op1=ALU.add,
         )
 
-        kT = keep.tile([P, CB, N_K], BF16)
+        kT = keep.tile([P, CB // 2, N_K], F32)
         v_codes = keep.tile([P, NG, C], U32, align_bytes=64)
         v_scales = keep.tile([P, NG, C], U8, align_bytes=64)
         w_codes = keep.tile([P, NF, C], U32, align_bytes=64)
@@ -121,9 +119,11 @@ def tile_epipolarcrossattention_pa_kernel(tc, Q, K, V, kpts_L, kpts_R, Wm, bm, o
         qT = {}
         far_v = {}
         far_u = {}
-        cap = {}
+        far = {}
         y = {}
-        chunk_max = {}
+        half_min = {}
+        total = {}
+        inverse = {}
         exp_bias = {}
         e = {}
         half_sum = {}
@@ -155,17 +155,26 @@ def tile_epipolarcrossattention_pa_kernel(tc, Q, K, V, kpts_L, kpts_R, Wm, bm, o
             steps = []
             for b in range(4):
                 m0 = j * BANK + b * P
+                words = k_raw[j][:, b, :].bitcast(F32)
+                copy = nc.vector.tensor_copy if b % 2 == 0 else nc.scalar.copy
                 steps.extend(turning(
-                    [k_raw[j][:, b, cb * P:(cb + 1) * P] for cb in range(CB)], ident_bf[:], 4,
-                    lambda bank, m0=m0: nc.vector.tensor_copy(out=kT[:, :, m0:m0 + P], in_=bank[:]),
+                    [words[:, u * P:(u + 1) * P] for u in range(CB // 2)], ident_f32[:], 2,
+                    lambda bank, m0=m0, copy=copy: copy(out=kT[:, :, m0:m0 + P], in_=bank[:]),
                 ))
             return steps
 
         def turn_queries(i):
             qT[i] = two.tile([P, CB, P], BF16, name="qT")
+            words = q_raw[i][:].bitcast(F32)
             return turning(
-                [q_raw[i][:, cb * P:(cb + 1) * P] for cb in range(CB)], ident_bf[:], 2,
-                lambda bank: nc.scalar.copy(out=qT[i][:], in_=bank[:]),
+                [words[:, u * P:(u + 1) * P] for u in range(CB // 2)], ident_f32[:], 1,
+                lambda bank: nc.scalar.activation(
+                    out=qT[i][:].rearrange("p (u e) n -> p u e n", e=2),
+                    in_=bank[:].rearrange("p u n -> p (u n)").bitcast(BF16).rearrange(
+                        "p (u n e) -> p u e n", n=P, e=2
+                    ),
+                    func=ACT.Copy, scale=SHRINK,
+                ),
             )
 
         def turn_weights(f, pair):
@@ -220,22 +229,20 @@ def tile_epipolarcrossattention_pa_kernel(tc, Q, K, V, kpts_L, kpts_R, Wm, bm, o
 
         def caps(i, h):
             if h == 0:
-                cap[i] = two.tile([P, N_K], BF16, name="cap")
+                far[i] = two.tile([P, N_K], BF16, name="far")
             cols = slice(h * HALF, (h + 1) * HALF)
             nc.vector.tensor_tensor(
-                out=cap[i][:, cols], in0=far_v[i, h][:], in1=far_u[i, h][:], op=ALU.max
-            )
-            nc.vector.tensor_scalar(
-                out=cap[i][:, cols], in0=cap[i][:, cols], scalar1=REACH, scalar2=0.5,
-                op0=ALU.is_lt, op1=ALU.subtract,
+                out=far[i][:, cols], in0=far_v[i, h][:], in1=far_u[i, h][:], op=ALU.max
             )
 
         def scores(i, j, steps):
             cols = slice(j * BANK, (j + 1) * BANK)
             bank = ps_score.tile([P, BANK], F32, tag="score")
             for cb in range(CB):
+                u, odd = cb // 2, cb % 2
                 nc.tensor.matmul(
-                    out=bank[:], lhsT=qT[i][:, cb, :], rhs=kT[:, cb, cols],
+                    out=bank[:], lhsT=qT[i][:, cb, :],
+                    rhs=kT[:, u, cols].bitcast(BF16)[:, odd::2],
                     start=(cb == 0), stop=(cb == CB - 1),
                 )
                 if cb < len(steps):
@@ -245,22 +252,25 @@ def tile_epipolarcrossattention_pa_kernel(tc, Q, K, V, kpts_L, kpts_R, Wm, bm, o
         def masked(i, j):
             if j == 0:
                 y[i] = two.tile([P, N_K], F32, name="y")
-                chunk_max[i] = two.tile([P, NJ], F32, name="chunk_max")
             cols = slice(j * BANK, (j + 1) * BANK)
             nc.vector.scalar_tensor_tensor(
-                out=y[i][:, cols], in0=score_bank[i, j][:], scalar=SHRINK, in1=cap[i][:, cols],
-                op0=ALU.mult, op1=ALU.min,
+                out=y[i][:, cols], in0=far[i][:, cols], scalar=REACH, in1=score_bank[i, j][:],
+                op0=ALU.is_ge, op1=ALU.subtract,
             )
+
+        def lowest(i, h):
+            if h == 0:
+                half_min[i] = two.tile([P, 2], F32, name="half_min")
             nc.vector.tensor_reduce(
-                out=chunk_max[i][:, j:j + 1], in_=y[i][:, cols], axis=AXIS.X, op=ALU.max
+                out=half_min[i][:, h:h + 1], in_=y[i][:, h * HALF:(h + 1) * HALF],
+                axis=AXIS.X, op=ALU.min,
             )
 
         def row_max(i):
-            top = two.tile([P, 1], F32, name="top")
-            nc.vector.tensor_reduce(out=top[:], in_=chunk_max[i][:], axis=AXIS.X, op=ALU.max)
             exp_bias[i] = two.tile([P, 1], F32, name="exp_bias")
             nc.vector.tensor_scalar(
-                out=exp_bias[i][:], in0=top[:], scalar1=-GROW, scalar2=None, op0=ALU.mult
+                out=exp_bias[i][:], in0=half_min[i][:, 0:1], scalar1=half_min[i][:, 1:2],
+                scalar2=GROW, op0=ALU.min, op1=ALU.mult,
             )
 
         def exponentials(i):
@@ -270,18 +280,23 @@ def tile_epipolarcrossattention_pa_kernel(tc, Q, K, V, kpts_L, kpts_R, Wm, bm, o
                 cols = slice(h * HALF, (h + 1) * HALF)
                 nc.scalar.activation(
                     out=e[i][:, cols], in_=y[i][:, cols], func=ACT.Exp,
-                    bias=exp_bias[i][:, 0:1], scale=GROW, accum_out=half_sum[i][:, h:h + 1],
+                    bias=exp_bias[i][:, 0:1], scale=-GROW, accum_out=half_sum[i][:, h:h + 1],
                 )
             e_grouped[i] = two.tile([P, N_K], BF16, name="e_grouped", align_bytes=64)
 
-        def normaliser(i):
-            total = two.tile([P, 1], F32, name="total")
-            nc.vector.tensor_reduce(out=total[:], in_=half_sum[i][:], axis=AXIS.X, op=ALU.add)
-            inverse = two.tile([P, 1], F32, name="inverse")
-            nc.vector.reciprocal(out=inverse[:], in_=total[:])
+        def row_sum(i):
+            total[i] = two.tile([P, 1], F32, name="total")
+            nc.vector.tensor_reduce(out=total[i][:], in_=half_sum[i][:], axis=AXIS.X, op=ALU.add)
+
+        def inverse_sum(i):
+            inverse[i] = two.tile([P, 1], F32, name="inverse")
+            nc.vector.reciprocal(out=inverse[i][:], in_=total[i][:])
+
+        def spread_inverse(i):
             spread[i] = two.tile([P, P], F32, name="spread")
             nc.vector.tensor_scalar(
-                out=spread[i][:], in0=ones[:], scalar1=inverse[:, 0:1], scalar2=None, op0=ALU.mult
+                out=spread[i][:], in0=ones[:], scalar1=inverse[i][:, 0:1], scalar2=None,
+                op0=ALU.mult,
             )
 
         def quantise_e(i):
@@ -375,74 +390,96 @@ def tile_epipolarcrossattention_pa_kernel(tc, Q, K, V, kpts_L, kpts_R, Wm, bm, o
             live = i < NT
             more = i + 1 < NT
             steps = [[], [], [], []]
-            if i == 0:
-                steps = [turn_keys(1), turn_keys(2), turn_keys(3), []]
             if 2 <= i:
                 steps[0] = turn_e(i - 2)
-            if 2 <= i and live:
-                normaliser(i - 2)
-                steps[3] = turn_inv_sum(i - 2)
+            if 3 <= i:
+                steps[3] = turn_inv_sum(i - 3)
             if more:
                 distances(i + 1, 0)
             if live:
                 scores(i, 0, steps[0])
             else:
                 run(steps[0])
-            if 1 <= i <= NT:
+            if i <= NT:
                 exponentials(i - 1)
-            if i == 0:
-                caps(0, 0)
             if live:
                 masked(i, 0)
-            if 2 <= i:
-                quantise_e(i - 2)
-            fill(i, 0)
-            if live:
-                scores(i, 1, steps[1] if i == 0 else steps[1] + (turn_queries(i + 1) if more else []))
-            else:
-                run(steps[1])
             if more:
                 caps(i + 1, 0)
-            if i == 0:
-                caps(0, 1)
+            fill(i, 0)
+            if live:
+                scores(i, 1, turn_queries(i + 1) if more else [])
+            if 2 <= i:
+                quantise_e(i - 2)
             if live:
                 masked(i, 1)
             fill(i, 1)
             if more:
                 distances(i + 1, 1)
-            if 1 <= i <= 2 * NF:
+            if i <= 2 * NF:
                 f, half = (i - 1) // 2, (i - 1) % 2
                 steps[2] = turn_weights(f, 2 * half) + turn_weights(f, 2 * half + 1)
             if live:
                 scores(i, 2, steps[2])
                 masked(i, 2)
+                lowest(i, 0)
             fill(i, 2)
-            if i == 0:
-                steps[3] = turn_queries(1)
             if live:
                 scores(i, 3, steps[3])
+            else:
+                run(steps[3])
+            if live:
                 masked(i, 3)
+                if 2 <= i:
+                    row_sum(i - 2)
+                if more:
+                    caps(i + 1, 1)
+                lowest(i, 1)
+                if 2 <= i:
+                    inverse_sum(i - 2)
                 row_max(i)
-            if more:
-                caps(i + 1, 1)
-            if 1 <= i <= 2 * NF and (i - 1) % 2 == 1:
+            if i <= 2 * NF and (i - 1) % 2 == 1:
                 quantise_weights((i - 1) // 2)
             fill(i, 3)
+            if 2 <= i and live:
+                spread_inverse(i - 2)
 
-        run(turn_queries(0) + turn_keys(0))
-        distances(0, 0)
-        distances(0, 1)
+        def first_round():
+            run(turn_queries(0) + turn_keys(0))
+            scores(0, 0, turn_keys(1))
+            distances(0, 0)
+            scores(0, 1, turn_keys(2))
+            caps(0, 0)
+            masked(0, 0)
+            distances(0, 1)
+            scores(0, 2, turn_keys(3))
+            masked(0, 1)
+            caps(0, 1)
+            distances(1, 0)
+            scores(0, 3, turn_queries(1))
+            masked(0, 2)
+            caps(1, 0)
+            distances(1, 1)
+            lowest(0, 0)
+            masked(0, 3)
+            caps(1, 1)
+            lowest(0, 1)
+            row_max(0)
+
         with tc.psum_pool(name="ps_score", bufs=4) as ps_score:
-            for i in range(NT + 1):
+            first_round()
+            for i in range(1, NT + 1):
                 softmax_round(i)
 
         with tc.psum_pool(name="ps_mx", bufs=4, reuse_waits="tile") as ps_mx:
             for i in range(NT + 1):
                 if i == 2:
-                    normaliser(NT - 2)
-                    normaliser(NT - 1)
+                    for step in (row_sum, inverse_sum, spread_inverse):
+                        step(NT - 2)
+                        step(NT - 1)
                 if i == 3:
-                    softmax_round(NT + 1)
+                    run(turn_e(NT - 1))
+                    quantise_e(NT - 1)
                     run(turn_inv_sum(NT - 2) + turn_inv_sum(NT - 1))
                 if i < NT:
                     attend(i)

@@ -24,6 +24,8 @@ K_PASS = 512
 NG = N_K // K_PASS
 NF = C // K_PASS
 HALF = N_K // 2
+KEYS_AHEAD = 3
+KEYS_SHARED = 10
 
 FLOPS = 2 * N_Q * N_K * C + 2 * N_Q * N_K * C + 2 * N_Q * C * C
 
@@ -43,6 +45,7 @@ def tile_epipolarcrossattention_pa_kernel(tc, Q, K, V, kpts_L, kpts_R, Wm, bm, o
         q_in = ctx.enter_context(tc.tile_pool(name="q_in", bufs=3))
         one = ctx.enter_context(tc.tile_pool(name="one", bufs=1))
         two = ctx.enter_context(tc.tile_pool(name="two", bufs=2))
+        three = ctx.enter_context(tc.tile_pool(name="three", bufs=3))
         ps_turn = ctx.enter_context(tc.psum_pool(name="ps_turn", bufs=4))
         ctx.enter_context(tc.manual_schedule())
 
@@ -61,35 +64,40 @@ def tile_epipolarcrossattention_pa_kernel(tc, Q, K, V, kpts_L, kpts_R, Wm, bm, o
             q_raw[i] = q_in.tile([P, C], BF16, name="q_raw")
             nc.sync.dma_start(out=q_raw[i][:], in_=q_rows[i])
 
+        def load_weights(h):
+            w_raw[h] = raw.tile([P, 4, C], BF16, name="w_raw", tag="raw")
+            nc.sync.dma_start(out=w_raw[h][:], in_=w_rows[h])
+
         def load_values(g):
             v_raw[g] = raw.tile([P, 4, C], BF16, name="v_raw", tag="raw")
             nc.sync.dma_start(
                 out=v_raw[g][:].rearrange("p (u e) c -> p u e c", u=2), in_=v_rows[g]
             )
 
+        load_queries(0)
         left = keep.tile([P, NT, 2], BF16)
         nc.sync.dma_start(out=left[:], in_=kpts_L.rearrange("(p i) c -> p i c", i=NT))
-        load_queries(0)
         right = keep.tile([P, N_K, 2], BF16)
         for j in range(NJ):
             k_raw[j] = raw.tile([P, 4, C], BF16, name="k_raw", tag="raw")
             for b in range(4):
                 nc.sync.dma_start(out=k_raw[j][:, b, :], in_=k_rows[j][:, b, :])
-            if j == 0:
+            if j == 2:
                 nc.sync.dma_start(
                     out=right[:].rearrange("p m c -> p (m c)"),
                     in_=kpts_R.rearrange("m c -> (m c)").partition_broadcast(P),
                 )
         load_queries(1)
-        for h in range(2):
-            w_raw[h] = raw.tile([P, 4, C], BF16, name="w_raw", tag="raw")
-            nc.sync.dma_start(out=w_raw[h][:], in_=w_rows[h])
+        load_values(0)
         load_queries(2)
-        for g in range(NG - 1):
+        for g in range(1, NG):
             load_values(g)
-        for i in range(3, NT):
+        load_queries(3)
+        load_weights(0)
+        load_queries(4)
+        load_weights(1)
+        for i in range(5, NT):
             load_queries(i)
-        load_values(NG - 1)
         bias = keep.tile([P, C], BF16)
         nc.sync.dma_start(out=bias[:], in_=bm.partition_broadcast(P))
 
@@ -151,17 +159,13 @@ def tile_epipolarcrossattention_pa_kernel(tc, Q, K, V, kpts_L, kpts_R, Wm, bm, o
 
             return [lambda s=s: step(s) for s in range(len(sources) // per_step)]
 
-        def turn_keys(j):
-            steps = []
-            for b in range(4):
-                m0 = j * BANK + b * P
-                words = k_raw[j][:, b, :].bitcast(F32)
-                copy = nc.vector.tensor_copy if b % 2 == 0 else nc.scalar.copy
-                steps.extend(turning(
-                    [words[:, u * P:(u + 1) * P] for u in range(CB // 2)], ident_f32[:], 2,
-                    lambda bank, m0=m0, copy=copy: copy(out=kT[:, :, m0:m0 + P], in_=bank[:]),
-                ))
-            return steps
+        def turn_keys(k):
+            words = k_raw[k // 4][:, k % 4, :].bitcast(F32)
+            copy = nc.scalar.copy if k % 2 == 1 and k < KEYS_SHARED else nc.vector.tensor_copy
+            return turning(
+                [words[:, u * P:(u + 1) * P] for u in range(CB // 2)], ident_f32[:], CB // 2,
+                lambda bank: copy(out=kT[:, :, k * P:(k + 1) * P], in_=bank[:]),
+            )
 
         def turn_queries(i):
             qT[i] = two.tile([P, CB, P], BF16, name="qT")
@@ -185,7 +189,8 @@ def tile_epipolarcrossattention_pa_kernel(tc, Q, K, V, kpts_L, kpts_R, Wm, bm, o
                 words = w_raw[block // 4][:, block % 4, :].bitcast(F32)
                 for u in range(2):
                     sources.append(words[:, (2 * f + u) * P:(2 * f + u + 1) * P])
-            return turning(sources, ident_f32[:], 1, lambda bank: nc.scalar.copy(
+            copy = nc.scalar.copy if pair % 2 == 0 else nc.vector.tensor_copy
+            return turning(sources, ident_f32[:], 1, lambda bank: copy(
                 out=w_grouped[f][:].bitcast(F32).rearrange("p (b o u) -> p b o u", o=P, u=2)[
                     :, 2 * pair:2 * pair + 2, :, :
                 ],
@@ -214,18 +219,25 @@ def tile_epipolarcrossattention_pa_kernel(tc, Q, K, V, kpts_L, kpts_R, Wm, bm, o
                 lambda bank: nc.scalar.copy(out=inv_sum[:, i, :], in_=bank[:, 0, :]),
             )
 
-        def distances(i, h):
+        def distance_v(i, h):
             cols = slice(h * HALF, (h + 1) * HALF)
             far_v[i, h] = two.tile([P, HALF], BF16, name="far_v")
             nc.scalar.activation(
                 out=far_v[i, h][:], in_=right[:, cols, 1], func=ACT.Abs,
                 bias=shift_v[:, i:i + 1], scale=V_STRETCH,
             )
+
+        def distance_u(i, h):
+            cols = slice(h * HALF, (h + 1) * HALF)
             far_u[i, h] = two.tile([P, HALF], BF16, name="far_u")
             nc.scalar.activation(
                 out=far_u[i, h][:], in_=right[:, cols, 0], func=ACT.Abs,
                 bias=shift_u[:, i:i + 1], scale=1.0,
             )
+
+        def distances(i, h):
+            distance_v(i, h)
+            distance_u(i, h)
 
         def caps(i, h):
             if h == 0:
@@ -293,7 +305,7 @@ def tile_epipolarcrossattention_pa_kernel(tc, Q, K, V, kpts_L, kpts_R, Wm, bm, o
             nc.vector.reciprocal(out=inverse[i][:], in_=total[i][:])
 
         def spread_inverse(i):
-            spread[i] = two.tile([P, P], F32, name="spread")
+            spread[i] = three.tile([P, P], F32, name="spread")
             nc.vector.tensor_scalar(
                 out=spread[i][:], in0=ones[:], scalar1=inverse[i][:, 0:1], scalar2=None,
                 op0=ALU.mult,
@@ -392,7 +404,7 @@ def tile_epipolarcrossattention_pa_kernel(tc, Q, K, V, kpts_L, kpts_R, Wm, bm, o
             steps = [[], [], [], []]
             if 2 <= i:
                 steps[0] = turn_e(i - 2)
-            if 3 <= i:
+            if 3 <= i and live:
                 steps[3] = turn_inv_sum(i - 3)
             if more:
                 distances(i + 1, 0)
@@ -407,8 +419,16 @@ def tile_epipolarcrossattention_pa_kernel(tc, Q, K, V, kpts_L, kpts_R, Wm, bm, o
             if more:
                 caps(i + 1, 0)
             fill(i, 0)
+            if more:
+                steps[1] = turn_queries(i + 1)
+            if 4 <= i < 7:
+                steps[2] = turn_weights((i - 4) // 2, 2 * (i % 2)) + turn_weights(
+                    (i - 4) // 2, 2 * (i % 2) + 1
+                )
+            if i == 7:
+                steps[1] = turn_weights(1, 2) + turn_weights(1, 3)
             if live:
-                scores(i, 1, turn_queries(i + 1) if more else [])
+                scores(i, 1, steps[1])
             if 2 <= i:
                 quantise_e(i - 2)
             if live:
@@ -416,19 +436,15 @@ def tile_epipolarcrossattention_pa_kernel(tc, Q, K, V, kpts_L, kpts_R, Wm, bm, o
             fill(i, 1)
             if more:
                 distances(i + 1, 1)
-            if i <= 2 * NF:
-                f, half = (i - 1) // 2, (i - 1) % 2
-                steps[2] = turn_weights(f, 2 * half) + turn_weights(f, 2 * half + 1)
             if live:
                 scores(i, 2, steps[2])
                 masked(i, 2)
                 lowest(i, 0)
             fill(i, 2)
+            if i == 7:
+                quantise_weights(1)
             if live:
                 scores(i, 3, steps[3])
-            else:
-                run(steps[3])
-            if live:
                 masked(i, 3)
                 if 2 <= i:
                     row_sum(i - 2)
@@ -438,33 +454,45 @@ def tile_epipolarcrossattention_pa_kernel(tc, Q, K, V, kpts_L, kpts_R, Wm, bm, o
                 if 2 <= i:
                     inverse_sum(i - 2)
                 row_max(i)
-            if i <= 2 * NF and (i - 1) % 2 == 1:
-                quantise_weights((i - 1) // 2)
+            if i == 5:
+                quantise_weights(0)
             fill(i, 3)
             if 2 <= i and live:
                 spread_inverse(i - 2)
 
         def first_round():
-            run(turn_queries(0) + turn_keys(0))
-            scores(0, 0, turn_keys(1))
-            distances(0, 0)
-            scores(0, 1, turn_keys(2))
-            caps(0, 0)
-            masked(0, 0)
-            distances(0, 1)
-            scores(0, 2, turn_keys(3))
-            masked(0, 1)
-            caps(0, 1)
-            distances(1, 0)
-            scores(0, 3, turn_queries(1))
-            masked(0, 2)
-            caps(1, 0)
-            distances(1, 1)
-            lowest(0, 0)
-            masked(0, 3)
-            caps(1, 1)
-            lowest(0, 1)
-            row_max(0)
+            after = {
+                6: [lambda: distance_v(0, 0)],
+                7: [lambda: distance_u(0, 0)],
+                8: [lambda: distance_v(0, 1)],
+                9: [lambda: distance_u(0, 1)],
+                10: turn_queries(1) + [lambda: caps(0, 0), lambda: masked(0, 0)],
+                11: [lambda: distance_v(1, 0), lambda: masked(0, 1)],
+                12: [lambda: distance_u(1, 0)],
+                13: [lambda: caps(0, 1), lambda: lowest(0, 0)],
+                14: [lambda: distance_v(1, 1), lambda: masked(0, 2)],
+                15: [
+                    lambda: distance_u(1, 1), lambda: masked(0, 3), lambda: caps(1, 0),
+                    lambda: lowest(0, 1), lambda: row_max(0), lambda: caps(1, 1),
+                ],
+            }
+            run(turn_queries(0))
+            for k in range(KEYS_AHEAD):
+                run(turn_keys(k))
+            for k in range(N_K // P):
+                if k + KEYS_AHEAD < N_K // P:
+                    run(turn_keys(k + KEYS_AHEAD))
+                j, b = divmod(k, BANK // P)
+                if b == 0:
+                    score_bank[0, j] = ps_score.tile([P, BANK], F32, name="bank", tag="score")
+                for cb in range(CB):
+                    u, odd = cb // 2, cb % 2
+                    nc.tensor.matmul(
+                        out=score_bank[0, j][:, b * P:(b + 1) * P], lhsT=qT[0][:, cb, :],
+                        rhs=kT[:, u, k * P:(k + 1) * P].bitcast(BF16)[:, odd::2],
+                        start=(cb == 0), stop=(cb == CB - 1),
+                    )
+                run(after.get(k, []))
 
         with tc.psum_pool(name="ps_score", bufs=4) as ps_score:
             first_round()
@@ -480,7 +508,8 @@ def tile_epipolarcrossattention_pa_kernel(tc, Q, K, V, kpts_L, kpts_R, Wm, bm, o
                 if i == 3:
                     run(turn_e(NT - 1))
                     quantise_e(NT - 1)
-                    run(turn_inv_sum(NT - 2) + turn_inv_sum(NT - 1))
+                    for last in range(NT - 3, NT):
+                        run(turn_inv_sum(last))
                 if i < NT:
                     attend(i)
                     quantise_matched(i)

@@ -41,7 +41,7 @@ def tile_epipolarcrossattention_pa_kernel(tc, Q, K, V, kpts_L, kpts_R, Wm, bm, o
     nc = tc.nc
     with ExitStack() as ctx:
         keep = ctx.enter_context(tc.tile_pool(name="keep", bufs=1))
-        raw = ctx.enter_context(tc.tile_pool(name="raw", bufs=5))
+        raw = ctx.enter_context(tc.tile_pool(name="raw", bufs=10))
         q_in = ctx.enter_context(tc.tile_pool(name="q_in", bufs=3))
         one = ctx.enter_context(tc.tile_pool(name="one", bufs=1))
         two = ctx.enter_context(tc.tile_pool(name="two", bufs=2))
@@ -51,9 +51,9 @@ def tile_epipolarcrossattention_pa_kernel(tc, Q, K, V, kpts_L, kpts_R, Wm, bm, o
 
         q_rows = Q.rearrange("(p i) c -> i p c", i=NT)
         out_rows = out.rearrange("(p i) o -> i p o", i=NT)
-        k_rows = K.rearrange("(j b p) c -> j p b c", b=4, p=P)
-        w_rows = Wm.rearrange("(h b p) c -> h p b c", b=4, p=P)
-        v_rows = V.rearrange("(g u q e) c -> g q u e c", u=2, q=P, e=2)
+        k_rows = K.rearrange("(k p) c -> k p c", p=P)
+        w_rows = Wm.rearrange("(h b p) c -> h p b c", b=2, p=P)
+        v_rows = V.rearrange("(g u q e) (f c) -> g f q u e c", u=2, q=P, e=2, f=NF)
 
         q_raw = {}
         k_raw = {}
@@ -61,41 +61,44 @@ def tile_epipolarcrossattention_pa_kernel(tc, Q, K, V, kpts_L, kpts_R, Wm, bm, o
         v_raw = {}
 
         def load_queries(i):
-            q_raw[i] = q_in.tile([P, C], BF16, name="q_raw")
+            q_raw[i] = q_in.tile([P, C], BF16, name="q_raw", tag="q_raw")
             nc.sync.dma_start(out=q_raw[i][:], in_=q_rows[i])
 
         def load_weights(h):
-            w_raw[h] = raw.tile([P, 4, C], BF16, name="w_raw", tag="raw")
+            w_raw[h] = raw.tile([P, 2, C], BF16, name="w_raw", tag="raw")
             nc.sync.dma_start(out=w_raw[h][:], in_=w_rows[h])
 
-        def load_values(g):
-            v_raw[g] = raw.tile([P, 4, C], BF16, name="v_raw", tag="raw")
-            nc.sync.dma_start(
-                out=v_raw[g][:].rearrange("p (u e) c -> p u e c", u=2), in_=v_rows[g]
-            )
+        def load_values(g, f):
+            v_raw[g, f] = raw.tile([P, 4, C // NF], BF16, name="v_raw", tag="raw")
+            for u in range(2):
+                nc.sync.dma_start(
+                    out=v_raw[g, f][:, 2 * u:2 * u + 2, :], in_=v_rows[g, f][:, u, :, :]
+                )
 
         load_queries(0)
         left = keep.tile([P, NT, 2], BF16)
         nc.sync.dma_start(out=left[:], in_=kpts_L.rearrange("(p i) c -> p i c", i=NT))
         right = keep.tile([P, N_K, 2], BF16)
-        for j in range(NJ):
-            k_raw[j] = raw.tile([P, 4, C], BF16, name="k_raw", tag="raw")
-            for b in range(4):
-                nc.sync.dma_start(out=k_raw[j][:, b, :], in_=k_rows[j][:, b, :])
-            if j == 2:
+        for k in range(N_K // P):
+            if k % 2 == 0:
+                k_raw[k // 2] = raw.tile([P, 2, C], BF16, name="k_raw", tag="raw")
+            nc.sync.dma_start(out=k_raw[k // 2][:, k % 2, :], in_=k_rows[k])
+            if k == 11:
                 nc.sync.dma_start(
                     out=right[:].rearrange("p m c -> p (m c)"),
                     in_=kpts_R.rearrange("m c -> (m c)").partition_broadcast(P),
                 )
         load_queries(1)
-        load_values(0)
+        load_values(0, 0)
         load_queries(2)
         for g in range(1, NG):
-            load_values(g)
+            load_values(g, 0)
         load_queries(3)
-        load_weights(0)
+        for h in range(4):
+            load_weights(h)
         load_queries(4)
-        load_weights(1)
+        for g in range(NG):
+            load_values(g, 1)
         for i in range(5, NT):
             load_queries(i)
         bias = keep.tile([P, C], BF16)
@@ -122,6 +125,8 @@ def tile_epipolarcrossattention_pa_kernel(tc, Q, K, V, kpts_L, kpts_R, Wm, bm, o
         w_scales = keep.tile([P, NF, C], U8, align_bytes=64)
         e_codes = keep.tile([P, NT, NG * P], U32, align_bytes=64)
         e_scales = keep.tile([P, NT, NG * P], U8, align_bytes=64)
+        m_codes = keep.tile([P, NT, NF, P], U32, align_bytes=64)
+        m_scales = keep.tile([P, NT, NF, P], U8, align_bytes=64)
         inv_sum = keep.tile([P, NT, P], F32)
 
         qT = {}
@@ -138,8 +143,7 @@ def tile_epipolarcrossattention_pa_kernel(tc, Q, K, V, kpts_L, kpts_R, Wm, bm, o
         spread = {}
         e_grouped = {}
         m_grouped = {}
-        m_codes = {}
-        m_scales = {}
+        finished = {}
         w_grouped = {}
         v_grouped = {}
         score_bank = {}
@@ -160,7 +164,7 @@ def tile_epipolarcrossattention_pa_kernel(tc, Q, K, V, kpts_L, kpts_R, Wm, bm, o
             return [lambda s=s: step(s) for s in range(len(sources) // per_step)]
 
         def turn_keys(k):
-            words = k_raw[k // 4][:, k % 4, :].bitcast(F32)
+            words = k_raw[k // 2][:, k % 2, :].bitcast(F32)
             copy = nc.scalar.copy if k % 2 == 1 and k < KEYS_SHARED else nc.vector.tensor_copy
             return turning(
                 [words[:, u * P:(u + 1) * P] for u in range(CB // 2)], ident_f32[:], CB // 2,
@@ -170,15 +174,21 @@ def tile_epipolarcrossattention_pa_kernel(tc, Q, K, V, kpts_L, kpts_R, Wm, bm, o
         def turn_queries(i):
             qT[i] = two.tile([P, CB, P], BF16, name="qT")
             words = q_raw[i][:].bitcast(F32)
+
+            def leave(bank):
+                pairs = qT[i][:].rearrange("p (u e) n -> p u e n", e=2)
+                turned = bank[:].rearrange("p u n -> p (u n)").bitcast(BF16).rearrange(
+                    "p (u n e) -> p u e n", n=P, e=2
+                )
+                if i % 2 == 0 or i == 1:
+                    nc.scalar.activation(out=pairs, in_=turned, func=ACT.Copy, scale=SHRINK)
+                else:
+                    nc.vector.tensor_scalar(
+                        out=pairs, in0=turned, scalar1=SHRINK, scalar2=None, op0=ALU.mult
+                    )
+
             return turning(
-                [words[:, u * P:(u + 1) * P] for u in range(CB // 2)], ident_f32[:], 1,
-                lambda bank: nc.scalar.activation(
-                    out=qT[i][:].rearrange("p (u e) n -> p u e n", e=2),
-                    in_=bank[:].rearrange("p u n -> p (u n)").bitcast(BF16).rearrange(
-                        "p (u n e) -> p u e n", n=P, e=2
-                    ),
-                    func=ACT.Copy, scale=SHRINK,
-                ),
+                [words[:, u * P:(u + 1) * P] for u in range(CB // 2)], ident_f32[:], 1, leave
             )
 
         def turn_weights(f, pair):
@@ -186,7 +196,7 @@ def tile_epipolarcrossattention_pa_kernel(tc, Q, K, V, kpts_L, kpts_R, Wm, bm, o
                 w_grouped[f] = one.tile([P, 4 * C], BF16, name="w_grouped", align_bytes=64)
             sources = []
             for block in (2 * pair, 2 * pair + 1):
-                words = w_raw[block // 4][:, block % 4, :].bitcast(F32)
+                words = w_raw[block // 2][:, block % 2, :].bitcast(F32)
                 for u in range(2):
                     sources.append(words[:, (2 * f + u) * P:(2 * f + u + 1) * P])
             copy = nc.scalar.copy if pair % 2 == 0 else nc.vector.tensor_copy
@@ -241,7 +251,7 @@ def tile_epipolarcrossattention_pa_kernel(tc, Q, K, V, kpts_L, kpts_R, Wm, bm, o
 
         def caps(i, h):
             if h == 0:
-                far[i] = two.tile([P, N_K], BF16, name="far")
+                far[i] = two.tile([P, N_K], BF16, name="far", tag="far")
             cols = slice(h * HALF, (h + 1) * HALF)
             nc.vector.tensor_tensor(
                 out=far[i][:, cols], in0=far_v[i, h][:], in1=far_u[i, h][:], op=ALU.max
@@ -316,18 +326,21 @@ def tile_epipolarcrossattention_pa_kernel(tc, Q, K, V, kpts_L, kpts_R, Wm, bm, o
                 out=e_codes[:, i, :].bitcast(FP8X4), scales=e_scales[:, i, :], in_=e_grouped[i][:]
             )
 
-        def group_values(g, a):
+        def group_values(g, f, a, copy):
             if a == 0:
-                v_grouped[g] = one.tile([P, C, 4], BF16, name="v_grouped", align_bytes=64)
-            nc.vector.tensor_copy(
-                out=v_grouped[g][:].rearrange("p (a e q) t -> p a e q t", a=4, e=2)[:, a],
-                in_=v_raw[g][:].rearrange("p t (a q e) -> p a e q t", a=4, e=2)[:, a],
+                v_grouped[g, f] = two.tile(
+                    [P, C // NF, 4], BF16, name="v_grouped", align_bytes=64
+                )
+            copy(
+                out=v_grouped[g, f][:].rearrange("p (a e q) t -> p a e q t", a=2, e=2)[:, a],
+                in_=v_raw[g, f][:].rearrange("p t (a q e) -> p a e q t", a=2, e=2)[:, a],
             )
 
-        def quantise_values(g):
+        def quantise_values(g, f):
+            cols = slice(f * (C // NF), (f + 1) * (C // NF))
             nc.vector.quantize_mx(
-                out=v_codes[:, g, :].bitcast(FP8X4), scales=v_scales[:, g, :],
-                in_=v_grouped[g][:].rearrange("p c t -> p (c t)"),
+                out=v_codes[:, g, cols].bitcast(FP8X4), scales=v_scales[:, g, cols],
+                in_=v_grouped[g, f][:].rearrange("p c t -> p (c t)"),
             )
 
         def quantise_weights(f):
@@ -335,130 +348,130 @@ def tile_epipolarcrossattention_pa_kernel(tc, Q, K, V, kpts_L, kpts_R, Wm, bm, o
                 out=w_codes[:, f, :].bitcast(FP8X4), scales=w_scales[:, f, :], in_=w_grouped[f][:]
             )
 
-        def attend(i):
-            m_grouped[i] = two.tile([P, NF, P, 4], BF16, name="m_grouped", align_bytes=64)
-            for f in range(NF):
-                bank = ps_mx.tile([P, 4, P], F32, tag="mx")
-                for t in range(4):
-                    c0 = (4 * f + t) * P
-                    for g in range(NG):
-                        nc.tensor.matmul_mx(
-                            out=bank[:, t, :],
-                            lhsT=v_codes[:, g, c0:c0 + P].bitcast(FP8X4),
-                            lhsT_scale=v_scales[:, g, c0:c0 + P],
-                            rhs=e_codes[:, i, g * P:(g + 1) * P].bitcast(FP8X4),
-                            rhs_scale=e_scales[:, i, g * P:(g + 1) * P],
-                            start=(g == 0), stop=(g == NG - 1),
-                        )
-                nc.vector.tensor_tensor(
-                    out=m_grouped[i][:, f, :, :],
-                    in0=bank[:].rearrange("p t n -> p n t"),
-                    in1=inv_sum[:, i, :].unsqueeze(2).to_broadcast([P, P, 4]),
-                    op=ALU.mult,
-                )
-
-        def quantise_matched(i):
-            m_codes[i] = two.tile([P, NF * P], U32, name="m_codes", align_bytes=64)
-            m_scales[i] = two.tile([P, NF * P], U8, name="m_scales", align_bytes=64)
-            nc.vector.quantize_mx(
-                out=m_codes[i][:].bitcast(FP8X4), scales=m_scales[i][:],
-                in_=m_grouped[i][:].rearrange("p f n t -> p (f n t)"),
+        def attend(i, f):
+            m_grouped[i, f] = two.tile([P, P, 4], BF16, name="m_grouped", align_bytes=64)
+            bank = ps_mx.tile([P, 4, P], F32, tag="mx")
+            for t in range(4):
+                c0 = (4 * f + t) * P
+                for g in range(NG):
+                    nc.tensor.matmul_mx(
+                        out=bank[:, t, :],
+                        lhsT=v_codes[:, g, c0:c0 + P].bitcast(FP8X4),
+                        lhsT_scale=v_scales[:, g, c0:c0 + P],
+                        rhs=e_codes[:, i, g * P:(g + 1) * P].bitcast(FP8X4),
+                        rhs_scale=e_scales[:, i, g * P:(g + 1) * P],
+                        start=(g == 0), stop=(g == NG - 1),
+                    )
+            nc.vector.tensor_tensor(
+                out=m_grouped[i, f][:],
+                in0=bank[:].rearrange("p t n -> p n t"),
+                in1=inv_sum[:, i, :].unsqueeze(2).to_broadcast([P, P, 4]),
+                op=ALU.mult,
             )
 
-        def project(i):
-            result = two.tile([P, C], F32, name="result")
-            for h in range(C // BANK):
-                cols = slice(h * BANK, (h + 1) * BANK)
-                bank = ps_mx.tile([P, BANK], F32, tag="mx")
-                for f in range(NF):
-                    nc.tensor.matmul_mx(
-                        out=bank[:],
-                        lhsT=m_codes[i][:, f * P:(f + 1) * P].bitcast(FP8X4),
-                        lhsT_scale=m_scales[i][:, f * P:(f + 1) * P],
-                        rhs=w_codes[:, f, cols].bitcast(FP8X4),
-                        rhs_scale=w_scales[:, f, cols],
-                        start=(f == 0), stop=(f == NF - 1),
-                    )
-                nc.vector.tensor_tensor(
-                    out=result[:, cols], in0=bank[:], in1=bias[:, cols], op=ALU.add
+        def quantise_matched(i, f):
+            nc.vector.quantize_mx(
+                out=m_codes[:, i, f, :].bitcast(FP8X4), scales=m_scales[:, i, f, :],
+                in_=m_grouped[i, f][:].rearrange("p n t -> p (n t)"),
+            )
+
+        def project(i, h):
+            cols = slice(h * BANK, (h + 1) * BANK)
+            bank = ps_mx.tile([P, BANK], F32, tag="mx")
+            for f in range(NF):
+                nc.tensor.matmul_mx(
+                    out=bank[:],
+                    lhsT=m_codes[:, i, f, :].bitcast(FP8X4), lhsT_scale=m_scales[:, i, f, :],
+                    rhs=w_codes[:, f, cols].bitcast(FP8X4), rhs_scale=w_scales[:, f, cols],
+                    start=(f == 0), stop=(f == NF - 1),
                 )
-                nc.sync.dma_start(out=out_rows[i][:, cols], in_=result[:, cols])
+            if h == 0 and i < NT - 2:
+                result = two.tile([P, BANK], F32, name="result", tag="far")
+                nc.scalar.copy(out=result[:], in_=bank[:])
+                nc.gpsimd.tensor_tensor(
+                    out=result[:], in0=result[:], in1=bias[:, cols], op=ALU.add
+                )
+            else:
+                result = q_in.tile([P, BANK], F32, name="result", tag="q_raw")
+                nc.vector.tensor_tensor(out=result[:], in0=bank[:], in1=bias[:, cols], op=ALU.add)
+            finished[i, h] = result
+
+        def store(i, h):
+            nc.sync.dma_start(
+                out=out_rows[i][:, h * BANK:(h + 1) * BANK], in_=finished[i, h][:]
+            )
 
         def run(steps):
             for step in steps:
                 step()
 
-        background = []
-        for g in range(NG):
-            background.extend([lambda g=g, a=a: group_values(g, a) for a in range(4)])
-            background.append(lambda g=g: quantise_values(g))
+        early = []
+        late = []
+        for g, f in [(0, 0), (1, 0), (2, 0), (3, 0), (0, 1), (1, 1), (2, 1), (3, 1)]:
+            by_scalar = f == 1 and g > 1
+            copy = nc.scalar.copy if by_scalar else nc.vector.tensor_copy
+            for a in range(2):
+                (late if by_scalar else early).append(
+                    lambda g=g, f=f, a=a, copy=copy: group_values(g, f, a, copy)
+                )
+            if not by_scalar:
+                early.append(lambda g=g, f=f: quantise_values(g, f))
 
-        def fill(i, j):
-            item = NJ * (i - 1) + j
-            if 0 <= item < len(background):
-                background[item]()
+        def fill(i, s):
+            item = 3 * (i - 1) + s
+            if item < len(early):
+                early[item]()
 
         def softmax_round(i):
-            live = i < NT
             more = i + 1 < NT
-            steps = [[], [], [], []]
-            if 2 <= i:
-                steps[0] = turn_e(i - 2)
-            if 3 <= i and live:
-                steps[3] = turn_inv_sum(i - 3)
             if more:
                 distances(i + 1, 0)
-            if live:
-                scores(i, 0, steps[0])
-            else:
-                run(steps[0])
-            if i <= NT:
-                exponentials(i - 1)
-            if live:
-                masked(i, 0)
+            scores(i, 0, turn_e(i - 2) if i >= 2 else [])
+            exponentials(i - 1)
+            masked(i, 0)
             if more:
                 caps(i + 1, 0)
+            else:
+                late[0]()
+            scores(i, 1, turn_queries(i + 1) if more else [])
             fill(i, 0)
-            if more:
-                steps[1] = turn_queries(i + 1)
-            if 4 <= i < 7:
-                steps[2] = turn_weights((i - 4) // 2, 2 * (i % 2)) + turn_weights(
-                    (i - 4) // 2, 2 * (i % 2) + 1
-                )
-            if i == 7:
-                steps[1] = turn_weights(1, 2) + turn_weights(1, 3)
-            if live:
-                scores(i, 1, steps[1])
-            if 2 <= i:
+            if i >= 2:
                 quantise_e(i - 2)
-            if live:
-                masked(i, 1)
-            fill(i, 1)
+            masked(i, 1)
             if more:
                 distances(i + 1, 1)
-            if live:
-                scores(i, 2, steps[2])
-                masked(i, 2)
-                lowest(i, 0)
-            fill(i, 2)
-            if i == 7:
-                quantise_weights(1)
-            if live:
-                scores(i, 3, steps[3])
-                masked(i, 3)
-                if 2 <= i:
-                    row_sum(i - 2)
-                if more:
-                    caps(i + 1, 1)
-                lowest(i, 1)
-                if 2 <= i:
-                    inverse_sum(i - 2)
-                row_max(i)
-            if i == 5:
-                quantise_weights(0)
-            fill(i, 3)
-            if 2 <= i and live:
+            else:
+                late[1]()
+                late[2]()
+            f, half = (i - 3) // 2, (i - 3) % 2
+            scores(
+                i, 2,
+                turn_weights(f, 2 * half) + turn_weights(f, 2 * half + 1) if 0 <= f < NF else [],
+            )
+            masked(i, 2)
+            lowest(i, 0)
+            fill(i, 1)
+            scores(i, 3, turn_inv_sum(i - 3) if i >= 3 else [])
+            if not more:
+                row_sum(NT - 2)
+                quantise_values(2, 1)
+            masked(i, 3)
+            if i >= 2:
+                row_sum(i - 2)
+            if more:
+                caps(i + 1, 1)
+            lowest(i, 1)
+            if i >= 2:
+                inverse_sum(i - 2)
+            row_max(i)
+            if 0 <= f < NF and half == 1:
+                quantise_weights(f)
+            if i >= 2:
                 spread_inverse(i - 2)
+            fill(i, 2)
+            if not more:
+                inverse_sum(NT - 2)
+                spread_inverse(NT - 2)
 
         def first_round():
             after = {
@@ -496,22 +509,51 @@ def tile_epipolarcrossattention_pa_kernel(tc, Q, K, V, kpts_L, kpts_R, Wm, bm, o
 
         with tc.psum_pool(name="ps_score", bufs=4) as ps_score:
             first_round()
-            for i in range(1, NT + 1):
+            for i in range(1, NT):
                 softmax_round(i)
 
         with tc.psum_pool(name="ps_mx", bufs=4, reuse_waits="tile") as ps_mx:
+            last = NT - 1
+            run(turn_e(last - 1))
+            late[3]()
+            exponentials(last)
+            attend(0, 0)
+            attend(1, 0)
+            quantise_values(3, 1)
+            quantise_matched(0, 0)
+            attend(2, 0)
+            quantise_matched(1, 0)
+            attend(3, 0)
+            quantise_matched(2, 0)
             for i in range(NT + 1):
-                if i == 2:
-                    for step in (row_sum, inverse_sum, spread_inverse):
-                        step(NT - 2)
-                        step(NT - 1)
-                if i == 3:
-                    run(turn_e(NT - 1))
-                    quantise_e(NT - 1)
-                    for last in range(NT - 3, NT):
-                        run(turn_inv_sum(last))
                 if i < NT:
-                    attend(i)
-                    quantise_matched(i)
+                    attend(i, 1)
+                if i == 0:
+                    quantise_e(last - 1)
+                    run(turn_inv_sum(last - 2))
+                    run(turn_inv_sum(last - 1))
+                    quantise_matched(3, 0)
+                    row_sum(last)
+                elif i <= 4:
+                    quantise_matched(i + 3, 0)
+                if i == 1:
+                    run(turn_e(last))
+                    inverse_sum(last)
+                if i == 2:
+                    quantise_e(last)
+                    spread_inverse(last)
+                if i == 3:
+                    run(turn_inv_sum(last))
                 if i >= 1:
-                    project(i - 1)
+                    project(i - 1, 0)
+                if i < NT:
+                    quantise_matched(i, 1)
+                if i >= 1:
+                    if i - 1 >= NT - 2:
+                        store(i - 1, 0)
+                    project(i - 1, 1)
+                    store(i - 1, 1)
+                    if i - 1 < NT - 2:
+                        store(i - 1, 0)
+                if i + 4 < NT:
+                    attend(i + 4, 0)

@@ -83,10 +83,11 @@ def tile_epipolarcrossattention_pa_kernel(tc, Q, K, V, kpts_L, kpts_R, Wm, bm, o
             if k % 2 == 0:
                 k_raw[k // 2] = raw.tile([P, 2, C], BF16, name="k_raw", tag="raw")
             nc.sync.dma_start(out=k_raw[k // 2][:, k % 2, :], in_=k_rows[k])
-            if k == 11:
+            if k % 3 == 0 and k > 0 and k // 3 <= NJ:
+                m0 = (k // 3 - 1) * BANK
                 nc.sync.dma_start(
-                    out=right[:].rearrange("p m c -> p (m c)"),
-                    in_=kpts_R.rearrange("m c -> (m c)").partition_broadcast(P),
+                    out=right[:, m0:m0 + BANK, :].rearrange("p m c -> p (m c)"),
+                    in_=kpts_R[m0:m0 + BANK, :].rearrange("m c -> (m c)").partition_broadcast(P),
                 )
         load_queries(1)
         load_values(0, 0)
@@ -385,7 +386,7 @@ def tile_epipolarcrossattention_pa_kernel(tc, Q, K, V, kpts_L, kpts_R, Wm, bm, o
                     rhs=w_codes[:, f, cols].bitcast(FP8X4), rhs_scale=w_scales[:, f, cols],
                     start=(f == 0), stop=(f == NF - 1),
                 )
-            if h == 0 and i < NT - 2:
+            if h == 0 and i < NT - 1:
                 result = two.tile([P, BANK], F32, name="result", tag="far")
                 nc.scalar.copy(out=result[:], in_=bank[:])
                 nc.gpsimd.tensor_tensor(
@@ -525,16 +526,14 @@ def tile_epipolarcrossattention_pa_kernel(tc, Q, K, V, kpts_L, kpts_R, Wm, bm, o
             quantise_matched(1, 0)
             attend(3, 0)
             quantise_matched(2, 0)
-            for i in range(NT + 1):
-                if i < NT:
-                    attend(i, 1)
+            for i in range(last - 1):
+                attend(i, 1)
                 if i == 0:
                     quantise_e(last - 1)
                     run(turn_inv_sum(last - 2))
                     run(turn_inv_sum(last - 1))
-                    quantise_matched(3, 0)
                     row_sum(last)
-                elif i <= 4:
+                if i <= 4:
                     quantise_matched(i + 3, 0)
                 if i == 1:
                     run(turn_e(last))
@@ -546,14 +545,24 @@ def tile_epipolarcrossattention_pa_kernel(tc, Q, K, V, kpts_L, kpts_R, Wm, bm, o
                     run(turn_inv_sum(last))
                 if i >= 1:
                     project(i - 1, 0)
-                if i < NT:
-                    quantise_matched(i, 1)
+                quantise_matched(i, 1)
                 if i >= 1:
-                    if i - 1 >= NT - 2:
-                        store(i - 1, 0)
                     project(i - 1, 1)
                     store(i - 1, 1)
-                    if i - 1 < NT - 2:
-                        store(i - 1, 0)
+                    store(i - 1, 0)
                 if i + 4 < NT:
                     attend(i + 4, 0)
+            attend(last - 1, 1)
+            attend(last, 1)
+            quantise_matched(last - 1, 1)
+            quantise_matched(last, 1)
+            for i in (last - 2, last - 1):
+                project(i, 0)
+                project(i, 1)
+                store(i, 1)
+                if i == last - 1:
+                    project(last, 0)
+                    store(last, 0)
+                store(i, 0)
+            project(last, 1)
+            store(last, 1)

@@ -75,20 +75,17 @@ def tile_epipolarcrossattention_pa_kernel(tc, Q, K, V, kpts_L, kpts_R, Wm, bm, o
                     out=v_raw[g, f][:, 2 * u:2 * u + 2, :], in_=v_rows[g, f][:, u, :, :]
                 )
 
+        key_row = one.tile([P, 2 * N_K], BF16, name="key_row", tag="w_grouped", align_bytes=64)
+        nc.vector.memset(key_row[:].bitcast(U32), 0)
         load_queries(0)
+        nc.gpsimd.dma_start(out=key_row[0:1, :], in_=kpts_R.rearrange("(a m) c -> a (m c)", a=1))
         left = keep.tile([P, NT, 2], BF16)
         nc.sync.dma_start(out=left[:], in_=kpts_L.rearrange("(p i) c -> p i c", i=NT))
-        right = keep.tile([P, N_K, 2], BF16)
+        right = keep.tile([P, 2, N_K], BF16)
         for k in range(N_K // P):
             if k % 2 == 0:
                 k_raw[k // 2] = raw.tile([P, 2, C], BF16, name="k_raw", tag="raw")
             nc.sync.dma_start(out=k_raw[k // 2][:, k % 2, :], in_=k_rows[k])
-            if k % 3 == 0 and k > 0 and k // 3 <= NJ:
-                m0 = (k // 3 - 1) * BANK
-                nc.sync.dma_start(
-                    out=right[:, m0:m0 + BANK, :].rearrange("p m c -> p (m c)"),
-                    in_=kpts_R[m0:m0 + BANK, :].rearrange("m c -> (m c)").partition_broadcast(P),
-                )
         load_queries(1)
         load_values(0, 0)
         load_queries(2)
@@ -109,6 +106,8 @@ def tile_epipolarcrossattention_pa_kernel(tc, Q, K, V, kpts_L, kpts_R, Wm, bm, o
         make_identity(nc, ident_f32[:])
         ones = keep.tile([P, P], F32)
         nc.vector.memset(ones[:], 1.0)
+        ones_bf = keep.tile([P, P], BF16)
+        nc.vector.memset(ones_bf[:], 1.0)
         shift_v = keep.tile([P, NT], F32)
         nc.vector.tensor_scalar(
             out=shift_v[:], in0=left[:, :, 1], scalar1=-V_STRETCH, scalar2=None, op0=ALU.mult
@@ -194,7 +193,9 @@ def tile_epipolarcrossattention_pa_kernel(tc, Q, K, V, kpts_L, kpts_R, Wm, bm, o
 
         def turn_weights(f, pair):
             if pair == 0:
-                w_grouped[f] = one.tile([P, 4 * C], BF16, name="w_grouped", align_bytes=64)
+                w_grouped[f] = one.tile(
+                    [P, 4 * C], BF16, name="w_grouped", tag="w_grouped", align_bytes=64
+                )
             sources = []
             for block in (2 * pair, 2 * pair + 1):
                 words = w_raw[block // 2][:, block % 2, :].bitcast(F32)
@@ -230,11 +231,21 @@ def tile_epipolarcrossattention_pa_kernel(tc, Q, K, V, kpts_L, kpts_R, Wm, bm, o
                 lambda bank: nc.scalar.copy(out=inv_sum[:, i, :], in_=bank[:, 0, :]),
             )
 
+        def spread_keypoints(n):
+            keys = slice(n * 2 * P, (n + 1) * 2 * P)
+            bank = ps_turn.tile([P, BANK], F32, name="turned", tag="turn")
+            nc.tensor.matmul(
+                out=bank[:], lhsT=ones_bf[:], rhs=key_row[:, n * BANK:(n + 1) * BANK],
+                start=True, stop=True,
+            )
+            copy = nc.vector.tensor_copy if n % 2 == 0 else nc.scalar.copy
+            copy(out=right[:, :, keys], in_=bank[:].rearrange("p (m c) -> p c m", c=2))
+
         def distance_v(i, h):
             cols = slice(h * HALF, (h + 1) * HALF)
             far_v[i, h] = two.tile([P, HALF], BF16, name="far_v")
             nc.scalar.activation(
-                out=far_v[i, h][:], in_=right[:, cols, 1], func=ACT.Abs,
+                out=far_v[i, h][:], in_=right[:, 1, cols], func=ACT.Abs,
                 bias=shift_v[:, i:i + 1], scale=V_STRETCH,
             )
 
@@ -242,7 +253,7 @@ def tile_epipolarcrossattention_pa_kernel(tc, Q, K, V, kpts_L, kpts_R, Wm, bm, o
             cols = slice(h * HALF, (h + 1) * HALF)
             far_u[i, h] = two.tile([P, HALF], BF16, name="far_u")
             nc.scalar.activation(
-                out=far_u[i, h][:], in_=right[:, cols, 0], func=ACT.Abs,
+                out=far_u[i, h][:], in_=right[:, 0, cols], func=ACT.Abs,
                 bias=shift_u[:, i:i + 1], scale=1.0,
             )
 
@@ -475,16 +486,17 @@ def tile_epipolarcrossattention_pa_kernel(tc, Q, K, V, kpts_L, kpts_R, Wm, bm, o
                 spread_inverse(NT - 2)
 
         def first_round():
-            after = {
-                6: [lambda: distance_v(0, 0)],
-                7: [lambda: distance_u(0, 0)],
-                8: [lambda: distance_v(0, 1)],
-                9: [lambda: distance_u(0, 1)],
-                10: turn_queries(1) + [lambda: caps(0, 0), lambda: masked(0, 0)],
-                11: [lambda: distance_v(1, 0), lambda: masked(0, 1)],
+            after = {n: [lambda n=n: spread_keypoints(n)] for n in range(2 * N_K // BANK)}
+            later = {
+                4: [lambda: distance_v(0, 0)],
+                6: [lambda: distance_u(0, 0)],
+                8: [lambda: distance_v(0, 1), lambda: caps(0, 0), lambda: masked(0, 0)],
+                9: [lambda: distance_u(0, 1), lambda: masked(0, 1)],
+                10: turn_queries(1),
+                11: [lambda: distance_v(1, 0), lambda: caps(0, 1), lambda: masked(0, 2)],
                 12: [lambda: distance_u(1, 0)],
-                13: [lambda: caps(0, 1), lambda: lowest(0, 0)],
-                14: [lambda: distance_v(1, 1), lambda: masked(0, 2)],
+                13: [lambda: lowest(0, 0)],
+                14: [lambda: distance_v(1, 1)],
                 15: [
                     lambda: distance_u(1, 1), lambda: masked(0, 3), lambda: caps(1, 0),
                     lambda: lowest(0, 1), lambda: row_max(0), lambda: caps(1, 1),
@@ -507,6 +519,7 @@ def tile_epipolarcrossattention_pa_kernel(tc, Q, K, V, kpts_L, kpts_R, Wm, bm, o
                         start=(cb == 0), stop=(cb == CB - 1),
                     )
                 run(after.get(k, []))
+                run(later.get(k, []))
 
         with tc.psum_pool(name="ps_score", bufs=4) as ps_score:
             first_round()

@@ -76,9 +76,7 @@ def tile_epipolarcrossattention_pa_kernel(tc, Q, K, V, kpts_L, kpts_R, Wm, bm, o
                 )
 
         key_row = one.tile([P, 2 * N_K], BF16, name="key_row", tag="w_grouped", align_bytes=64)
-        nc.vector.memset(key_row[:].bitcast(U32), 0)
         load_queries(0)
-        nc.gpsimd.dma_start(out=key_row[0:1, :], in_=kpts_R.rearrange("(a m) c -> a (m c)", a=1))
         left = keep.tile([P, NT, 2], BF16)
         nc.sync.dma_start(out=left[:], in_=kpts_L.rearrange("(p i) c -> p i c", i=NT))
         right = keep.tile([P, 2, N_K], BF16)
@@ -104,6 +102,9 @@ def tile_epipolarcrossattention_pa_kernel(tc, Q, K, V, kpts_L, kpts_R, Wm, bm, o
 
         ident_f32 = keep.tile([P, P], F32)
         make_identity(nc, ident_f32[:])
+        nc.vector.memset(key_row[:, :N_K].bitcast(U32), 0)
+        nc.gpsimd.memset(key_row[:, N_K:].bitcast(U32), 0)
+        nc.gpsimd.dma_start(out=key_row[0:1, :], in_=kpts_R.rearrange("(a m) c -> a (m c)", a=1))
         ones = keep.tile([P, P], F32)
         nc.vector.memset(ones[:], 1.0)
         ones_bf = keep.tile([P, P], BF16)

@@ -24,6 +24,7 @@ K_PASS = 512
 NG = N_K // K_PASS
 NF = C // K_PASS
 HALF = N_K // 2
+WARM_UP = 5
 KEYS_AHEAD = 3
 KEYS_SHARED = 10
 
@@ -42,7 +43,7 @@ def tile_epipolarcrossattention_pa_kernel(tc, Q, K, V, kpts_L, kpts_R, Wm, bm, o
     with ExitStack() as ctx:
         keep = ctx.enter_context(tc.tile_pool(name="keep", bufs=1))
         raw = ctx.enter_context(tc.tile_pool(name="raw", bufs=10))
-        q_in = ctx.enter_context(tc.tile_pool(name="q_in", bufs=3))
+        q_in = ctx.enter_context(tc.tile_pool(name="q_in", bufs=4))
         one = ctx.enter_context(tc.tile_pool(name="one", bufs=1))
         two = ctx.enter_context(tc.tile_pool(name="two", bufs=2))
         three = ctx.enter_context(tc.tile_pool(name="three", bufs=3))
@@ -75,7 +76,10 @@ def tile_epipolarcrossattention_pa_kernel(tc, Q, K, V, kpts_L, kpts_R, Wm, bm, o
                     out=v_raw[g, f][:, 2 * u:2 * u + 2, :], in_=v_rows[g, f][:, u, :, :]
                 )
 
+        idle = keep.tile([P, BANK], BF16)
+        nc.vector.memset(idle[:].bitcast(U32), 0)
         key_row = one.tile([P, 2 * N_K], BF16, name="key_row", tag="w_grouped", align_bytes=64)
+        nc.vector.memset(key_row[:].bitcast(U32), 0)
         load_queries(0)
         left = keep.tile([P, NT, 2], BF16)
         nc.sync.dma_start(out=left[:], in_=kpts_L.rearrange("(p i) c -> p i c", i=NT))
@@ -84,6 +88,10 @@ def tile_epipolarcrossattention_pa_kernel(tc, Q, K, V, kpts_L, kpts_R, Wm, bm, o
             if k % 2 == 0:
                 k_raw[k // 2] = raw.tile([P, 2, C], BF16, name="k_raw", tag="raw")
             nc.sync.dma_start(out=k_raw[k // 2][:, k % 2, :], in_=k_rows[k])
+            if k == 5:
+                nc.sync.dma_start(
+                    out=key_row[0:1, :], in_=kpts_R.rearrange("(a m) c -> a (m c)", a=1)
+                )
         load_queries(1)
         load_values(0, 0)
         load_queries(2)
@@ -102,9 +110,6 @@ def tile_epipolarcrossattention_pa_kernel(tc, Q, K, V, kpts_L, kpts_R, Wm, bm, o
 
         ident_f32 = keep.tile([P, P], F32)
         make_identity(nc, ident_f32[:])
-        nc.vector.memset(key_row[:, :N_K].bitcast(U32), 0)
-        nc.gpsimd.memset(key_row[:, N_K:].bitcast(U32), 0)
-        nc.gpsimd.dma_start(out=key_row[0:1, :], in_=kpts_R.rearrange("(a m) c -> a (m c)", a=1))
         ones = keep.tile([P, P], F32)
         nc.vector.memset(ones[:], 1.0)
         ones_bf = keep.tile([P, P], BF16)
@@ -140,7 +145,6 @@ def tile_epipolarcrossattention_pa_kernel(tc, Q, K, V, kpts_L, kpts_R, Wm, bm, o
         inverse = {}
         exp_bias = {}
         e = {}
-        half_sum = {}
         spread = {}
         e_grouped = {}
         m_grouped = {}
@@ -202,8 +206,7 @@ def tile_epipolarcrossattention_pa_kernel(tc, Q, K, V, kpts_L, kpts_R, Wm, bm, o
                 words = w_raw[block // 2][:, block % 2, :].bitcast(F32)
                 for u in range(2):
                     sources.append(words[:, (2 * f + u) * P:(2 * f + u + 1) * P])
-            copy = nc.scalar.copy if pair % 2 == 0 else nc.vector.tensor_copy
-            return turning(sources, ident_f32[:], 1, lambda bank: copy(
+            return turning(sources, ident_f32[:], 1, lambda bank: nc.scalar.copy(
                 out=w_grouped[f][:].bitcast(F32).rearrange("p (b o u) -> p b o u", o=P, u=2)[
                     :, 2 * pair:2 * pair + 2, :, :
                 ],
@@ -310,18 +313,12 @@ def tile_epipolarcrossattention_pa_kernel(tc, Q, K, V, kpts_L, kpts_R, Wm, bm, o
 
         def exponentials(i):
             e[i] = two.tile([P, N_K], BF16, name="e")
-            half_sum[i] = two.tile([P, 2], F32, name="half_sum")
-            for h in range(2):
-                cols = slice(h * HALF, (h + 1) * HALF)
-                nc.scalar.activation(
-                    out=e[i][:, cols], in_=y[i][:, cols], func=ACT.Exp,
-                    bias=exp_bias[i][:, 0:1], scale=-GROW, accum_out=half_sum[i][:, h:h + 1],
-                )
-            e_grouped[i] = two.tile([P, N_K], BF16, name="e_grouped", align_bytes=64)
-
-        def row_sum(i):
             total[i] = two.tile([P, 1], F32, name="total")
-            nc.vector.tensor_reduce(out=total[i][:], in_=half_sum[i][:], axis=AXIS.X, op=ALU.add)
+            nc.scalar.activation(
+                out=e[i][:], in_=y[i][:], func=ACT.Exp,
+                bias=exp_bias[i][:, 0:1], scale=-GROW, accum_out=total[i][:],
+            )
+            e_grouped[i] = two.tile([P, N_K], BF16, name="e_grouped", align_bytes=64)
 
         def inverse_sum(i):
             inverse[i] = two.tile([P, 1], F32, name="inverse")
@@ -329,9 +326,9 @@ def tile_epipolarcrossattention_pa_kernel(tc, Q, K, V, kpts_L, kpts_R, Wm, bm, o
 
         def spread_inverse(i):
             spread[i] = three.tile([P, P], F32, name="spread")
-            nc.vector.tensor_scalar(
-                out=spread[i][:], in0=ones[:], scalar1=inverse[i][:, 0:1], scalar2=None,
-                op0=ALU.mult,
+            nc.gpsimd.tensor_scalar(
+                out=spread[i][:], in0=ones[:], scalar1=inverse[i][:, 0:1], scalar2=0.0,
+                op0=ALU.mult, op1=ALU.add,
             )
 
         def quantise_e(i):
@@ -466,36 +463,40 @@ def tile_epipolarcrossattention_pa_kernel(tc, Q, K, V, kpts_L, kpts_R, Wm, bm, o
             fill(i, 1)
             scores(i, 3, turn_inv_sum(i - 3) if i >= 3 else [])
             if not more:
-                row_sum(NT - 2)
+                inverse_sum(NT - 2)
                 quantise_values(2, 1)
             masked(i, 3)
             if i >= 2:
-                row_sum(i - 2)
+                inverse_sum(i - 2)
             if more:
                 caps(i + 1, 1)
             lowest(i, 1)
-            if i >= 2:
-                inverse_sum(i - 2)
             row_max(i)
-            if 0 <= f < NF and half == 1:
-                quantise_weights(f)
+            if i == 4:
+                quantise_weights(0)
             if i >= 2:
                 spread_inverse(i - 2)
             fill(i, 2)
             if not more:
-                inverse_sum(NT - 2)
                 spread_inverse(NT - 2)
 
+        def keep_warm(count):
+            bank = ps_turn.tile([P, BANK], F32, name="warm", tag="turn")
+            for n in range(count):
+                nc.tensor.matmul(out=bank[:], lhsT=idle[:, :P], rhs=idle[:], start=True, stop=True)
+
         def first_round():
-            after = {n: [lambda n=n: spread_keypoints(n)] for n in range(2 * N_K // BANK)}
+            after = {3 + n // 2: [] for n in range(8)}
+            for n in range(8):
+                after[3 + n // 2].append(lambda n=n: spread_keypoints(n))
             later = {
-                4: [lambda: distance_v(0, 0)],
+                5: [lambda: distance_v(0, 0)],
                 6: [lambda: distance_u(0, 0)],
-                8: [lambda: distance_v(0, 1), lambda: caps(0, 0), lambda: masked(0, 0)],
-                9: [lambda: distance_u(0, 1), lambda: masked(0, 1)],
-                10: turn_queries(1),
-                11: [lambda: distance_v(1, 0), lambda: caps(0, 1), lambda: masked(0, 2)],
-                12: [lambda: distance_u(1, 0)],
+                8: [lambda: distance_v(0, 1)],
+                9: [lambda: distance_u(0, 1), lambda: caps(0, 0), lambda: masked(0, 0)],
+                10: turn_queries(1) + [lambda: masked(0, 1)],
+                11: [lambda: distance_v(1, 0), lambda: caps(0, 1)],
+                12: [lambda: distance_u(1, 0), lambda: masked(0, 2)],
                 13: [lambda: lowest(0, 0)],
                 14: [lambda: distance_v(1, 1)],
                 15: [
@@ -503,8 +504,10 @@ def tile_epipolarcrossattention_pa_kernel(tc, Q, K, V, kpts_L, kpts_R, Wm, bm, o
                     lambda: lowest(0, 1), lambda: row_max(0), lambda: caps(1, 1),
                 ],
             }
+            keep_warm(WARM_UP)
             run(turn_queries(0))
             for k in range(KEYS_AHEAD):
+                keep_warm(1)
                 run(turn_keys(k))
             for k in range(N_K // P):
                 if k + KEYS_AHEAD < N_K // P:
@@ -539,6 +542,7 @@ def tile_epipolarcrossattention_pa_kernel(tc, Q, K, V, kpts_L, kpts_R, Wm, bm, o
             attend(2, 0)
             quantise_matched(1, 0)
             attend(3, 0)
+            quantise_weights(1)
             quantise_matched(2, 0)
             for i in range(last - 1):
                 attend(i, 1)
@@ -546,15 +550,14 @@ def tile_epipolarcrossattention_pa_kernel(tc, Q, K, V, kpts_L, kpts_R, Wm, bm, o
                     quantise_e(last - 1)
                     run(turn_inv_sum(last - 2))
                     run(turn_inv_sum(last - 1))
-                    row_sum(last)
+                    inverse_sum(last)
                 if i <= 4:
                     quantise_matched(i + 3, 0)
                 if i == 1:
                     run(turn_e(last))
-                    inverse_sum(last)
+                    spread_inverse(last)
                 if i == 2:
                     quantise_e(last)
-                    spread_inverse(last)
                 if i == 3:
                     run(turn_inv_sum(last))
                 if i >= 1:

from contextlib import ExitStack

import concourse.mybir as mybir
from concourse.masks import make_identity

BF16 = mybir.dt.bfloat16
F32 = mybir.dt.float32
U32 = mybir.dt.uint32
U8 = mybir.dt.uint8
FP8X4 = mybir.dt.float8_e4m3fn_x4
ALU = mybir.AluOpType
ACT = mybir.ActivationFunctionType
AXIS = mybir.AxisListType

P = 128
N_Q = 1024
N_K = 2048
C = 1024
NT = N_Q // P
CB = C // P
BANK = 512
NJ = N_K // BANK
K_PASS = 512
NG = N_K // K_PASS
NF = C // K_PASS
HALF = N_K // 2
WARM_UP = 5
KEYS_AHEAD = 3
KEYS_SHARED = 10

FLOPS = 2 * N_Q * N_K * C + 2 * N_Q * N_K * C + 2 * N_Q * C * C

V_TOL = 3.0
MAX_DISP = 192.0
REACH = MAX_DISP / 2.0
V_STRETCH = REACH / V_TOL
SHRINK = 2.0 ** -72
GROW = 2.0 ** 67


def tile_epipolarcrossattention_pa_kernel(tc, Q, K, V, kpts_L, kpts_R, Wm, bm, out):
    nc = tc.nc
    with ExitStack() as ctx:
        keep = ctx.enter_context(tc.tile_pool(name="keep", bufs=1))
        raw = ctx.enter_context(tc.tile_pool(name="raw", bufs=10))
        q_in = ctx.enter_context(tc.tile_pool(name="q_in", bufs=4))
        one = ctx.enter_context(tc.tile_pool(name="one", bufs=1))
        two = ctx.enter_context(tc.tile_pool(name="two", bufs=2))
        three = ctx.enter_context(tc.tile_pool(name="three", bufs=3))
        ps_turn = ctx.enter_context(tc.psum_pool(name="ps_turn", bufs=4))
        ctx.enter_context(tc.manual_schedule())

        q_rows = Q.rearrange("(p i) c -> i p c", i=NT)
        out_rows = out.rearrange("(p i) o -> i p o", i=NT)
        k_rows = K.rearrange("(k p) c -> k p c", p=P)
        w_rows = Wm.rearrange("(h b p) c -> h p b c", b=2, p=P)
        v_rows = V.rearrange("(g u q e) (f c) -> g f q u e c", u=2, q=P, e=2, f=NF)

        q_raw = {}
        k_raw = {}
        w_raw = {}
        v_raw = {}

        def load_queries(i):
            q_raw[i] = q_in.tile([P, C], BF16, name="q_raw", tag="q_raw")
            nc.sync.dma_start(out=q_raw[i][:], in_=q_rows[i])

        def load_weights(h):
            w_raw[h] = raw.tile([P, 2, C], BF16, name="w_raw", tag="raw")
            nc.sync.dma_start(out=w_raw[h][:], in_=w_rows[h])

        def load_values(g, f):
            v_raw[g, f] = raw.tile([P, 4, C // NF], BF16, name="v_raw", tag="raw")
            for u in range(2):
                nc.sync.dma_start(
                    out=v_raw[g, f][:, 2 * u:2 * u + 2, :], in_=v_rows[g, f][:, u, :, :]
                )

        idle = keep.tile([P, BANK], BF16)
        nc.vector.memset(idle[:].bitcast(U32), 0)
        key_row = one.tile([P, 2 * N_K], BF16, name="key_row", tag="w_grouped", align_bytes=64)
        nc.vector.memset(key_row[:].bitcast(U32), 0)
        load_queries(0)
        left = keep.tile([P, NT, 2], BF16)
        nc.sync.dma_start(out=left[:], in_=kpts_L.rearrange("(p i) c -> p i c", i=NT))
        right = keep.tile([P, 2, N_K], BF16)
        for k in range(N_K // P):
            if k % 2 == 0:
                k_raw[k // 2] = raw.tile([P, 2, C], BF16, name="k_raw", tag="raw")
            nc.sync.dma_start(out=k_raw[k // 2][:, k % 2, :], in_=k_rows[k])
            if k == 5:
                nc.sync.dma_start(
                    out=key_row[0:1, :], in_=kpts_R.rearrange("(a m) c -> a (m c)", a=1)
                )
        load_queries(1)
        load_values(0, 0)
        load_queries(2)
        for g in range(1, NG):
            load_values(g, 0)
        load_queries(3)
        for h in range(4):
            load_weights(h)
        load_queries(4)
        for g in range(NG):
            load_values(g, 1)
        for i in range(5, NT):
            load_queries(i)
        bias = keep.tile([P, C], BF16)
        nc.sync.dma_start(out=bias[:], in_=bm.partition_broadcast(P))

        ident_f32 = keep.tile([P, P], F32)
        make_identity(nc, ident_f32[:])
        ones = keep.tile([P, P], F32)
        nc.vector.memset(ones[:], 1.0)
        ones_bf = keep.tile([P, P], BF16)
        nc.vector.memset(ones_bf[:], 1.0)
        shift_v = keep.tile([P, NT], F32)
        nc.vector.tensor_scalar(
            out=shift_v[:], in0=left[:, :, 1], scalar1=-V_STRETCH, scalar2=None, op0=ALU.mult
        )
        shift_u = keep.tile([P, NT], F32)
        nc.vector.tensor_scalar(
            out=shift_u[:], in0=left[:, :, 0], scalar1=-1.0, scalar2=REACH,
            op0=ALU.mult, op1=ALU.add,
        )

        kT = keep.tile([P, CB // 2, N_K], F32)
        v_codes = keep.tile([P, NG, C], U32, align_bytes=64)
        v_scales = keep.tile([P, NG, C], U8, align_bytes=64)
        w_codes = keep.tile([P, NF, C], U32, align_bytes=64)
        w_scales = keep.tile([P, NF, C], U8, align_bytes=64)
        e_codes = keep.tile([P, NT, NG * P], U32, align_bytes=64)
        e_scales = keep.tile([P, NT, NG * P], U8, align_bytes=64)
        m_codes = keep.tile([P, NT, NF, P], U32, align_bytes=64)
        m_scales = keep.tile([P, NT, NF, P], U8, align_bytes=64)
        inv_sum = keep.tile([P, NT, P], F32)

        qT = {}
        far_v = {}
        far_u = {}
        far = {}
        y = {}
        half_min = {}
        total = {}
        inverse = {}
        exp_bias = {}
        e = {}
        spread = {}
        e_grouped = {}
        m_grouped = {}
        finished = {}
        w_grouped = {}
        v_grouped = {}
        score_bank = {}

        def turning(sources, identity, per_step, leave):
            held = {}

            def step(s):
                if s == 0:
                    held[0] = ps_turn.tile(
                        [P, len(sources), P], identity.dtype, name="turned", tag="turn"
                    )
                for t in range(s * per_step, (s + 1) * per_step):
                    nc.tensor.transpose(held[0][:, t, :], sources[t], identity)
                if (s + 1) * per_step == len(sources):
                    leave(held[0])

            return [lambda s=s: step(s) for s in range(len(sources) // per_step)]

        def turn_keys(k):
            words = k_raw[k // 2][:, k % 2, :].bitcast(F32)
            copy = nc.scalar.copy if k % 2 == 1 and k < KEYS_SHARED else nc.vector.tensor_copy
            return turning(
                [words[:, u * P:(u + 1) * P] for u in range(CB // 2)], ident_f32[:], CB // 2,
                lambda bank: copy(out=kT[:, :, k * P:(k + 1) * P], in_=bank[:]),
            )

        def turn_queries(i):
            qT[i] = two.tile([P, CB, P], BF16, name="qT")
            words = q_raw[i][:].bitcast(F32)

            def leave(bank):
                pairs = qT[i][:].rearrange("p (u e) n -> p u e n", e=2)
                turned = bank[:].rearrange("p u n -> p (u n)").bitcast(BF16).rearrange(
                    "p (u n e) -> p u e n", n=P, e=2
                )
                if i % 2 == 0 or i == 1:
                    nc.scalar.activation(out=pairs, in_=turned, func=ACT.Copy, scale=SHRINK)
                else:
                    nc.vector.tensor_scalar(
                        out=pairs, in0=turned, scalar1=SHRINK, scalar2=None, op0=ALU.mult
                    )

            return turning(
                [words[:, u * P:(u + 1) * P] for u in range(CB // 2)], ident_f32[:], 1, leave
            )

        def turn_weights(f, pair):
            if pair == 0:
                w_grouped[f] = one.tile(
                    [P, 4 * C], BF16, name="w_grouped", tag="w_grouped", align_bytes=64
                )
            sources = []
            for block in (2 * pair, 2 * pair + 1):
                words = w_raw[block // 2][:, block % 2, :].bitcast(F32)
                for u in range(2):
                    sources.append(words[:, (2 * f + u) * P:(2 * f + u + 1) * P])
            return turning(sources, ident_f32[:], 1, lambda bank: nc.scalar.copy(
                out=w_grouped[f][:].bitcast(F32).rearrange("p (b o u) -> p b o u", o=P, u=2)[
                    :, 2 * pair:2 * pair + 2, :, :
                ],
                in_=bank[:].rearrange("p (b u) o -> p b o u", u=2),
            ))

        def turn_e(i):
            words = e[i][:].bitcast(F32)
            steps = []
            for pair in range(2):
                steps.extend(turning(
                    [words[:, (4 * pair + t) * P:(4 * pair + t + 1) * P] for t in range(4)],
                    ident_f32[:], 1,
                    lambda bank, pair=pair: nc.scalar.copy(
                        out=e_grouped[i][:].bitcast(F32).rearrange(
                            "p (g n u) -> p g n u", g=NG, u=2
                        )[:, 2 * pair:2 * pair + 2, :, :],
                        in_=bank[:].rearrange("p (g u) n -> p g n u", u=2),
                    ),
                ))
            return steps

        def turn_inv_sum(i):
            return turning(
                [spread[i][:]], ident_f32[:], 1,
                lambda bank: nc.scalar.copy(out=inv_sum[:, i, :], in_=bank[:, 0, :]),
            )

        def spread_keypoints(n):
            keys = slice(n * 2 * P, (n + 1) * 2 * P)
            bank = ps_turn.tile([P, BANK], F32, name="turned", tag="turn")
            nc.tensor.matmul(
                out=bank[:], lhsT=ones_bf[:], rhs=key_row[:, n * BANK:(n + 1) * BANK],
                start=True, stop=True,
            )
            copy = nc.vector.tensor_copy if n % 2 == 0 else nc.scalar.copy
            copy(out=right[:, :, keys], in_=bank[:].rearrange("p (m c) -> p c m", c=2))

        def distance_v(i, h):
            cols = slice(h * HALF, (h + 1) * HALF)
            far_v[i, h] = two.tile([P, HALF], BF16, name="far_v")
            nc.scalar.activation(
                out=far_v[i, h][:], in_=right[:, 1, cols], func=ACT.Abs,
                bias=shift_v[:, i:i + 1], scale=V_STRETCH,
            )

        def distance_u(i, h):
            cols = slice(h * HALF, (h + 1) * HALF)
            far_u[i, h] = two.tile([P, HALF], BF16, name="far_u")
            nc.scalar.activation(
                out=far_u[i, h][:], in_=right[:, 0, cols], func=ACT.Abs,
                bias=shift_u[:, i:i + 1], scale=1.0,
            )

        def distances(i, h):
            distance_v(i, h)
            distance_u(i, h)

        def caps(i, h):
            if h == 0:
                far[i] = two.tile([P, N_K], BF16, name="far", tag="far")
            cols = slice(h * HALF, (h + 1) * HALF)
            nc.vector.tensor_tensor(
                out=far[i][:, cols], in0=far_v[i, h][:], in1=far_u[i, h][:], op=ALU.max
            )

        def scores(i, j, steps):
            cols = slice(j * BANK, (j + 1) * BANK)
            bank = ps_score.tile([P, BANK], F32, tag="score")
            for cb in range(CB):
                u, odd = cb // 2, cb % 2
                nc.tensor.matmul(
                    out=bank[:], lhsT=qT[i][:, cb, :],
                    rhs=kT[:, u, cols].bitcast(BF16)[:, odd::2],
                    start=(cb == 0), stop=(cb == CB - 1),
                )
                if cb < len(steps):
                    steps[cb]()
            score_bank[i, j] = bank

        def masked(i, j):
            if j == 0:
                y[i] = two.tile([P, N_K], F32, name="y")
            cols = slice(j * BANK, (j + 1) * BANK)
            nc.vector.scalar_tensor_tensor(
                out=y[i][:, cols], in0=far[i][:, cols], scalar=REACH, in1=score_bank[i, j][:],
                op0=ALU.is_ge, op1=ALU.subtract,
            )

        def lowest(i, h):
            if h == 0:
                half_min[i] = two.tile([P, 2], F32, name="half_min")
            nc.vector.tensor_reduce(
                out=half_min[i][:, h:h + 1], in_=y[i][:, h * HALF:(h + 1) * HALF],
                axis=AXIS.X, op=ALU.min,
            )

        def row_max(i):
            exp_bias[i] = two.tile([P, 1], F32, name="exp_bias")
            nc.vector.tensor_scalar(
                out=exp_bias[i][:], in0=half_min[i][:, 0:1], scalar1=half_min[i][:, 1:2],
                scalar2=GROW, op0=ALU.min, op1=ALU.mult,
            )

        def exponentials(i):
            e[i] = two.tile([P, N_K], BF16, name="e")
            total[i] = two.tile([P, 1], F32, name="total")
            nc.scalar.activation(
                out=e[i][:], in_=y[i][:], func=ACT.Exp,
                bias=exp_bias[i][:, 0:1], scale=-GROW, accum_out=total[i][:],
            )
            e_grouped[i] = two.tile([P, N_K], BF16, name="e_grouped", align_bytes=64)

        def inverse_sum(i):
            inverse[i] = two.tile([P, 1], F32, name="inverse")
            nc.vector.reciprocal(out=inverse[i][:], in_=total[i][:])

        def spread_inverse(i):
            spread[i] = three.tile([P, P], F32, name="spread")
            nc.gpsimd.tensor_scalar(
                out=spread[i][:], in0=ones[:], scalar1=inverse[i][:, 0:1], scalar2=0.0,
                op0=ALU.mult, op1=ALU.add,
            )

        def quantise_e(i):
            nc.vector.quantize_mx(
                out=e_codes[:, i, :].bitcast(FP8X4), scales=e_scales[:, i, :], in_=e_grouped[i][:]
            )

        def group_values(g, f, a, copy):
            if a == 0:
                v_grouped[g, f] = two.tile(
                    [P, C // NF, 4], BF16, name="v_grouped", align_bytes=64
                )
            copy(
                out=v_grouped[g, f][:].rearrange("p (a e q) t -> p a e q t", a=2, e=2)[:, a],
                in_=v_raw[g, f][:].rearrange("p t (a q e) -> p a e q t", a=2, e=2)[:, a],
            )

        def quantise_values(g, f):
            cols = slice(f * (C // NF), (f + 1) * (C // NF))
            nc.vector.quantize_mx(
                out=v_codes[:, g, cols].bitcast(FP8X4), scales=v_scales[:, g, cols],
                in_=v_grouped[g, f][:].rearrange("p c t -> p (c t)"),
            )

        def quantise_weights(f):
            nc.vector.quantize_mx(
                out=w_codes[:, f, :].bitcast(FP8X4), scales=w_scales[:, f, :], in_=w_grouped[f][:]
            )

        def attend(i, f):
            m_grouped[i, f] = two.tile([P, P, 4], BF16, name="m_grouped", align_bytes=64)
            bank = ps_mx.tile([P, 4, P], F32, tag="mx")
            for t in range(4):
                c0 = (4 * f + t) * P
                for g in range(NG):
                    nc.tensor.matmul_mx(
                        out=bank[:, t, :],
                        lhsT=v_codes[:, g, c0:c0 + P].bitcast(FP8X4),
                        lhsT_scale=v_scales[:, g, c0:c0 + P],
                        rhs=e_codes[:, i, g * P:(g + 1) * P].bitcast(FP8X4),
                        rhs_scale=e_scales[:, i, g * P:(g + 1) * P],
                        start=(g == 0), stop=(g == NG - 1),
                    )
            nc.vector.tensor_tensor(
                out=m_grouped[i, f][:],
                in0=bank[:].rearrange("p t n -> p n t"),
                in1=inv_sum[:, i, :].unsqueeze(2).to_broadcast([P, P, 4]),
                op=ALU.mult,
            )

        def quantise_matched(i, f):
            nc.vector.quantize_mx(
                out=m_codes[:, i, f, :].bitcast(FP8X4), scales=m_scales[:, i, f, :],
                in_=m_grouped[i, f][:].rearrange("p n t -> p (n t)"),
            )

        def project(i, h):
            cols = slice(h * BANK, (h + 1) * BANK)
            bank = ps_mx.tile([P, BANK], F32, tag="mx")
            for f in range(NF):
                nc.tensor.matmul_mx(
                    out=bank[:],
                    lhsT=m_codes[:, i, f, :].bitcast(FP8X4), lhsT_scale=m_scales[:, i, f, :],
                    rhs=w_codes[:, f, cols].bitcast(FP8X4), rhs_scale=w_scales[:, f, cols],
                    start=(f == 0), stop=(f == NF - 1),
                )
            if h == 0 and i < NT - 1:
                result = two.tile([P, BANK], F32, name="result", tag="far")
                nc.scalar.copy(out=result[:], in_=bank[:])
                nc.gpsimd.tensor_tensor(
                    out=result[:], in0=result[:], in1=bias[:, cols], op=ALU.add
                )
            else:
                result = q_in.tile([P, BANK], F32, name="result", tag="q_raw")
                nc.vector.tensor_tensor(out=result[:], in0=bank[:], in1=bias[:, cols], op=ALU.add)
            finished[i, h] = result

        def store(i, h):
            nc.sync.dma_start(
                out=out_rows[i][:, h * BANK:(h + 1) * BANK], in_=finished[i, h][:]
            )

        def run(steps):
            for step in steps:
                step()

        early = []
        late = []
        for g, f in [(0, 0), (1, 0), (2, 0), (3, 0), (0, 1), (1, 1), (2, 1), (3, 1)]:
            by_scalar = f == 1 and g > 1
            copy = nc.scalar.copy if by_scalar else nc.vector.tensor_copy
            for a in range(2):
                (late if by_scalar else early).append(
                    lambda g=g, f=f, a=a, copy=copy: group_values(g, f, a, copy)
                )
            if not by_scalar:
                early.append(lambda g=g, f=f: quantise_values(g, f))

        def fill(i, s):
            item = 3 * (i - 1) + s
            if item < len(early):
                early[item]()

        def softmax_round(i):
            more = i + 1 < NT
            if more:
                distances(i + 1, 0)
            scores(i, 0, turn_e(i - 2) if i >= 2 else [])
            exponentials(i - 1)
            masked(i, 0)
            if more:
                caps(i + 1, 0)
            else:
                late[0]()
            scores(i, 1, turn_queries(i + 1) if more else [])
            fill(i, 0)
            if i >= 2:
                quantise_e(i - 2)
            masked(i, 1)
            if more:
                distances(i + 1, 1)
            else:
                late[1]()
                late[2]()
            f, half = (i - 3) // 2, (i - 3) % 2
            scores(
                i, 2,
                turn_weights(f, 2 * half) + turn_weights(f, 2 * half + 1) if 0 <= f < NF else [],
            )
            masked(i, 2)
            lowest(i, 0)
            fill(i, 1)
            scores(i, 3, turn_inv_sum(i - 3) if i >= 3 else [])
            if not more:
                inverse_sum(NT - 2)
                quantise_values(2, 1)
            masked(i, 3)
            if i >= 2:
                inverse_sum(i - 2)
            if more:
                caps(i + 1, 1)
            lowest(i, 1)
            row_max(i)
            if i == 4:
                quantise_weights(0)
            if i >= 2:
                spread_inverse(i - 2)
            fill(i, 2)
            if not more:
                spread_inverse(NT - 2)

        def keep_warm(count):
            bank = ps_turn.tile([P, BANK], F32, name="warm", tag="turn")
            for n in range(count):
                nc.tensor.matmul(out=bank[:], lhsT=idle[:, :P], rhs=idle[:], start=True, stop=True)

        def first_round():
            after = {3 + n // 2: [] for n in range(8)}
            for n in range(8):
                after[3 + n // 2].append(lambda n=n: spread_keypoints(n))
            later = {
                5: [lambda: distance_v(0, 0)],
                6: [lambda: distance_u(0, 0)],
                8: [lambda: distance_v(0, 1)],
                9: [lambda: distance_u(0, 1), lambda: caps(0, 0), lambda: masked(0, 0)],
                10: turn_queries(1) + [lambda: masked(0, 1)],
                11: [lambda: distance_v(1, 0), lambda: caps(0, 1)],
                12: [lambda: distance_u(1, 0), lambda: masked(0, 2)],
                13: [lambda: lowest(0, 0)],
                14: [lambda: distance_v(1, 1)],
                15: [
                    lambda: distance_u(1, 1), lambda: masked(0, 3), lambda: caps(1, 0),
                    lambda: lowest(0, 1), lambda: row_max(0), lambda: caps(1, 1),
                ],
            }
            keep_warm(WARM_UP)
            run(turn_queries(0))
            for k in range(KEYS_AHEAD):
                keep_warm(1)
                run(turn_keys(k))
            for k in range(N_K // P):
                if k + KEYS_AHEAD < N_K // P:
                    run(turn_keys(k + KEYS_AHEAD))
                j, b = divmod(k, BANK // P)
                if b == 0:
                    score_bank[0, j] = ps_score.tile([P, BANK], F32, name="bank", tag="score")
                for cb in range(CB):
                    u, odd = cb // 2, cb % 2
                    nc.tensor.matmul(
                        out=score_bank[0, j][:, b * P:(b + 1) * P], lhsT=qT[0][:, cb, :],
                        rhs=kT[:, u, k * P:(k + 1) * P].bitcast(BF16)[:, odd::2],
                        start=(cb == 0), stop=(cb == CB - 1),
                    )
                run(after.get(k, []))
                run(later.get(k, []))

        with tc.psum_pool(name="ps_score", bufs=4) as ps_score:
            first_round()
            for i in range(1, NT):
                softmax_round(i)

        with tc.psum_pool(name="ps_mx", bufs=4, reuse_waits="tile") as ps_mx:
            last = NT - 1
            run(turn_e(last - 1))
            late[3]()
            exponentials(last)
            attend(0, 0)
            attend(1, 0)
            quantise_values(3, 1)
            quantise_matched(0, 0)
            attend(2, 0)
            quantise_matched(1, 0)
            attend(3, 0)
            quantise_weights(1)
            quantise_matched(2, 0)
            for i in range(last - 1):
                attend(i, 1)
                if i == 0:
                    quantise_e(last - 1)
                    run(turn_inv_sum(last - 2))
                    run(turn_inv_sum(last - 1))
                    inverse_sum(last)
                if i <= 4:
                    quantise_matched(i + 3, 0)
                if i == 1:
                    run(turn_e(last))
                    spread_inverse(last)
                if i == 2:
                    quantise_e(last)
                if i == 3:
                    run(turn_inv_sum(last))
                if i >= 1:
                    project(i - 1, 0)
                quantise_matched(i, 1)
                if i >= 1:
                    project(i - 1, 1)
                    store(i - 1, 1)
                    store(i - 1, 0)
                if i + 4 < NT:
                    attend(i + 4, 0)
            attend(last - 1, 1)
            attend(last, 1)
            quantise_matched(last - 1, 1)
            quantise_matched(last, 1)
            for i in (last - 2, last - 1):
                project(i, 0)
                project(i, 1)
                store(i, 1)
                if i == last - 1:
                    project(last, 0)
                    store(last, 0)
                store(i, 0)
            project(last, 1)
            store(last, 1)
